import numpy as np
import ml_dtypes


def mxq(x, axis, fmt="e4m3"):
    dtype, down = {"e4m3": (ml_dtypes.float8_e4m3fn, 7), "e5m2": (ml_dtypes.float8_e5m2, 14)}[fmt]
    v = np.moveaxis(np.asarray(x, np.float32).astype(ml_dtypes.bfloat16).astype(np.float64), axis, -1)
    blocks = v.reshape(v.shape[:-1] + (-1, 32))
    amax = np.abs(blocks).max(-1, keepdims=True)
    byte = np.maximum(np.where(amax > 0, np.frexp(amax)[1] - 1 + 127, 0) - down, 1)
    scale = np.exp2(byte - 127.0)
    codes = (blocks / scale).astype(np.float32).astype(dtype).astype(np.float64)
    return np.moveaxis((codes * scale).reshape(v.shape), -1, axis)


WIDE = False


def mx_kscale(k):
    if not WIDE:
        return np.ones(k)
    levels = np.array([10, -10, 5, -5, 0])
    a = np.random.permutation(np.resize(levels, k // 512 * 4)).reshape(k // 512, 4)
    idx = np.arange(k)
    return np.exp2(a[idx // 512, idx % 128 // 32])


BF16 = ml_dtypes.bfloat16


def bf(x):
    return np.asarray(x, np.float32).astype(BF16)


def f64(x):
    return np.asarray(x).astype(np.float64)


B, D, H = 4096, 512, 512
M_SCALE = 1.5


def setup_inputs():
    s, t = mx_kscale(D), mx_kscale(H)
    return {'x': bf(np.random.standard_normal((B, D)) * s),
            'h_prev': bf(np.random.standard_normal((B, H)) * t),
            'c_prev': bf(np.random.standard_normal((B, H))),
            'W_ih': bf(np.random.standard_normal((2 * H, D)) * 0.7 / np.sqrt(D) / s[None, :]),
            'b_ih': bf(np.random.standard_normal(2 * H) * 0.2),
            'W_hh': bf(np.random.standard_normal((2 * H, H)) * 0.7 / np.sqrt(H) / t[None, :]),
            'b_hh': bf(np.random.standard_normal(2 * H) * 0.2),
            'log_lambda': bf(np.log(np.random.uniform(0.05, 0.5, H))),
            'z_bias': bf(np.random.standard_normal(H) * 0.2),
            'm_bias': bf(np.random.standard_normal(H) * 0.2)}


def reference(x, h_prev, c_prev, W_ih, b_ih, W_hh, b_hh, log_lambda, z_bias, m_bias):
    gates = ((mxq(f64(x), 1, 'e4m3') @ mxq(f64(W_ih), 1, 'e4m3').T) + f64(b_ih)
             + (mxq(f64(h_prev), 1, 'e4m3') @ mxq(f64(W_hh), 1, 'e4m3').T) + f64(b_hh))
    z_raw, m_raw = gates[:, :H], gates[:, H:]
    z_t = np.tanh(z_raw + f64(z_bias))
    M_t = M_SCALE * np.tanh(m_raw + f64(m_bias))
    A_base = -np.exp(f64(log_lambda))
    innov = z_t - M_t * (A_base * f64(c_prev))
    return z_t, M_t, innov

@@ -1,0 +1,158 @@
+from contextlib import ExitStack
+
+import concourse.mybir as mybir
+from concourse.masks import make_identity
+
+F32 = mybir.dt.float32
+BF16 = mybir.dt.bfloat16
+U32 = mybir.dt.uint32
+U8 = mybir.dt.uint8
+FP8X4 = mybir.dt.float8_e4m3fn_x4
+ACT = mybir.ActivationFunctionType
+ALU = mybir.AluOpType
+
+P = 128
+B, D, H = 4096, 512, 512
+NT = B // P
+TB = 4
+NB = NT // TB
+M_SCALE = 1.5
+FLOPS = 2 * B * (2 * H) * (D + H)
+LOAD_GROUPS = (4, 4, 8, 8, 8)
+
+
+def tile_koslmcell_pa_t_kernel(tc, x, h_prev, c_prev, W_ih, b_ih, W_hh, b_hh,
+                                          log_lambda, z_bias, m_bias, out_0, out_1, out_2):
+    nc = tc.nc
+    with ExitStack() as ctx:
+        const = ctx.enter_context(tc.tile_pool(name="const", bufs=1))
+        resid = ctx.enter_context(tc.tile_pool(name="resid", bufs=1))
+        gpool = ctx.enter_context(tc.tile_pool(name="gpool", bufs=4))
+        qpool = ctx.enter_context(tc.tile_pool(name="qpool", bufs=3))
+        stage = ctx.enter_context(tc.tile_pool(name="stage", bufs=3))
+        tpsum = ctx.enter_context(tc.psum_pool(name="tpsum", bufs=4))
+        apsum = ctx.enter_context(tc.psum_pool(name="apsum", bufs=4))
+
+        def row(v):
+            return v.rearrange("(o n) -> o n", o=1)
+
+        vecs = const.tile([P, 3 * H], BF16, name="vecs")
+        nc.vector.memset(vecs[:], 0.0)
+        ones = const.tile([P, P], BF16, name="ones")
+        nc.vector.memset(ones[:], 1.0)
+        nc.scalar.dma_start(out=vecs[0:1, 0:2 * H], in_=row(b_ih))
+        nc.scalar.dma_start(out=vecs[1:2, 0:2 * H], in_=row(b_hh))
+        nc.scalar.dma_start(out=vecs[2:3, 0:H], in_=row(z_bias))
+        nc.scalar.dma_start(out=vecs[2:3, H:2 * H], in_=row(m_bias))
+        nc.scalar.dma_start(out=vecs[0:1, 2 * H:3 * H], in_=row(log_lambda))
+        ident = const.tile([P, P], F32, name="ident")
+        make_identity(nc, ident[:])
+
+        wraw = []
+        for op, (w, tg) in enumerate(((W_ih, "zst"), (W_hh, "mst"))):
+            wr = stage.tile([P, 8 * D], BF16, name="wraw%d" % op, tag=tg)
+            nc.sync.dma_start(out=wr[:].rearrange("p (a k) -> p a k", k=D),
+                              in_=w.rearrange("(a p) k -> p a k", p=P))
+            wraw.append(wr)
+        views = [v.rearrange("(p t) k -> p t k", t=NT) for v in (x, h_prev, c_prev)]
+        where = [[], [], []]
+        t0 = 0
+        for g, n in enumerate(LOAD_GROUPS):
+            for i in range(3):
+                rt = resid.tile([P, n * D], BF16, name="in%d_%d" % (i, g))
+                nc.sync.dma_start(out=rt[:].rearrange("p (t k) -> p t k", k=D),
+                                  in_=views[i][:, t0:t0 + n, :])
+                for j in range(n):
+                    where[i].append((rt, j))
+            t0 += n
+        outs = [o.rearrange("(p t) n -> p t n", t=NT) for o in (out_0, out_1, out_2)]
+
+        bias = const.tile([P, 2 * H], F32, name="bias")
+        lam = const.tile([P, H], F32, name="lam")
+        for half in range(3):
+            bp = apsum.tile([P, H], F32, name="bp%d" % half, tag="acc")
+            nc.tensor.matmul(out=bp[:], lhsT=ones[:], rhs=vecs[:, half * H:(half + 1) * H],
+                             start=True, stop=True)
+            if half < 2:
+                nc.vector.tensor_copy(out=bias[:, half * H:(half + 1) * H], in_=bp[:])
+            else:
+                nc.scalar.activation(out=lam[:], in_=bp[:], func=ACT.Exp)
+
+        wq = const.tile([P, 2, 2 * H], U32, name="wq", align_bytes=64)
+        wsc = const.tile([P, 2, 2 * H], U8, name="wsc", align_bytes=64)
+
+        def transposes(srcs, label, engines):
+            grouped = gpool.tile([P, 4 * P, 2], F32, name="grp_" + label, tag="grp", align_bytes=64)
+            for half in range(2):
+                tp = tpsum.tile([P, 2, 2, P], F32, name="tp_%s_%d" % (label, half), tag="tp")
+                for a in range(2):
+                    for u in range(2):
+                        nc.tensor.transpose(tp[:, a, u, :], srcs[2 * half + a][:, u * P:(u + 1) * P], ident[:])
+                dst = grouped[:, 2 * P * half:2 * P * (half + 1), :].rearrange("p (a r) u -> p a r u", a=2)
+                src = tp[:].rearrange("p a u r -> p a r u")
+                if engines[half] == "s":
+                    nc.scalar.copy(out=dst, in_=src)
+                else:
+                    nc.vector.tensor_copy(out=dst, in_=src)
+            return grouped
+
+        def quantise(grouped, codes, scales):
+            nc.vector.quantize_mx(out=codes.bitcast(FP8X4), scales=scales,
+                                  in_=grouped[:].rearrange("p c u -> p (c u)").bitcast(BF16))
+
+        wg = []
+        for op in range(2):
+            wv = wraw[op][:].bitcast(F32)
+            for u in range(2):
+                srcs = [wv[:, (4 * u + a) * (D // 2):(4 * u + a + 1) * (D // 2)] for a in range(4)]
+                wg.append((transposes(srcs, "w%d%d" % (op, u), "sv"), op, u))
+        for g, op, u in wg:
+            quantise(g, wq[:, op, u * H:(u + 1) * H], wsc[:, op, u * H:(u + 1) * H])
+
+        def prep(b):
+            gs = []
+            for op in range(2):
+                srcs = []
+                for t in range(b * TB, (b + 1) * TB):
+                    rt, j = where[op][t]
+                    srcs.append(rt[:].bitcast(F32)[:, j * (D // 2):(j + 1) * (D // 2)])
+                gs.append(transposes(srcs, "b%d_%d" % (b, op), "ss"))
+            res = []
+            for op in range(2):
+                q = qpool.tile([P, TB * P], U32, name="q%d_%d" % (b, op), tag="q%d" % op, align_bytes=64)
+                s = qpool.tile([P, TB * P], U8, name="s%d_%d" % (b, op), tag="s%d" % op, align_bytes=64)
+                quantise(gs[op], q[:], s[:])
+                res.append((q, s))
+            return res
+
+        nxt = prep(0)
+        for b in range(NB):
+            cur = nxt
+            if b + 1 < NB:
+                nxt = prep(b + 1)
+            zst = stage.tile([P, TB, H], F32, name="zst%d" % b, tag="zst")
+            mst = stage.tile([P, TB, H], F32, name="mst%d" % b, tag="mst")
+            ist = stage.tile([P, TB, H], F32, name="ist%d" % b, tag="ist")
+            for i in range(TB):
+                ct, j = where[2][b * TB + i]
+                nc.gpsimd.tensor_tensor(out=ist[:, i, :], in0=ct[:, j * H:(j + 1) * H], in1=lam[:], op=ALU.mult)
+            for i in range(TB):
+                cols = slice(i * P, (i + 1) * P)
+                accs = [apsum.tile([P, H], F32, name="acc%d_%d_%d" % (b, i, half), tag="acc") for half in range(2)]
+                for op in range(2):
+                    q, s = cur[op]
+                    for half in range(2):
+                        nc.tensor.matmul_mx(out=accs[half][:],
+                                            lhsT=q[:, cols].bitcast(FP8X4), lhsT_scale=s[:, cols],
+                                            rhs=wq[:, op, half * H:(half + 1) * H].bitcast(FP8X4),
+                                            rhs_scale=wsc[:, op, half * H:(half + 1) * H],
+                                            start=(op == 0), stop=(op == 1))
+                nc.vector.tensor_tensor(out=zst[:, i, :], in0=accs[0][:], in1=bias[:, 0:H], op=ALU.add)
+                nc.vector.tensor_tensor(out=mst[:, i, :], in0=accs[1][:], in1=bias[:, H:2 * H], op=ALU.add)
+                nc.scalar.activation(out=zst[:, i, :], in_=zst[:, i, :], func=ACT.Tanh)
+                nc.scalar.activation(out=mst[:, i, :], in_=mst[:, i, :], func=ACT.Tanh)
+                nc.scalar.mul(out=mst[:, i, :], in_=mst[:, i, :], mul=M_SCALE)
+                nc.vector.tensor_tensor(out=ist[:, i, :], in0=ist[:, i, :], in1=mst[:, i, :], op=ALU.mult)
+                nc.vector.tensor_tensor(out=ist[:, i, :], in0=ist[:, i, :], in1=zst[:, i, :], op=ALU.add)
+            for o, st in zip(outs, (zst, mst, ist)):
+                nc.sync.dma_start(out=o[:, b * TB:(b + 1) * TB, :], in_=st[:])

@@ -18,7 +18,6 @@ TB = 4
 NB = NT // TB
 M_SCALE = 1.5
 FLOPS = 2 * B * (2 * H) * (D + H)
-LOAD_GROUPS = (4, 4, 8, 8, 8)
 
 
 def tile_koslmcell_pa_t_kernel(tc, x, h_prev, c_prev, W_ih, b_ih, W_hh, b_hh,
@@ -29,9 +28,10 @@ def tile_koslmcell_pa_t_kernel(tc, x, h_prev, c_prev, W_ih, b_ih, W_hh, b_hh,
         resid = ctx.enter_context(tc.tile_pool(name="resid", bufs=1))
         gpool = ctx.enter_context(tc.tile_pool(name="gpool", bufs=4))
         qpool = ctx.enter_context(tc.tile_pool(name="qpool", bufs=3))
+        tpool = ctx.enter_context(tc.tile_pool(name="tpool", bufs=4))
         stage = ctx.enter_context(tc.tile_pool(name="stage", bufs=3))
-        tpsum = ctx.enter_context(tc.psum_pool(name="tpsum", bufs=4))
-        apsum = ctx.enter_context(tc.psum_pool(name="apsum", bufs=4))
+        ps = ctx.enter_context(tc.psum_pool(name="ps", bufs=8))
+        ctx.enter_context(tc.manual_schedule())
 
         def row(v):
             return v.rearrange("(o n) -> o n", o=1)
@@ -48,35 +48,38 @@ def tile_koslmcell_pa_t_kernel(tc, x, h_prev, c_prev, W_ih, b_ih, W_hh, b_hh,
         ident = const.tile([P, P], F32, name="ident")
         make_identity(nc, ident[:])
 
-        wraw = []
-        for op, (w, tg) in enumerate(((W_ih, "zst"), (W_hh, "mst"))):
-            wr = stage.tile([P, 8 * D], BF16, name="wraw%d" % op, tag=tg)
-            nc.sync.dma_start(out=wr[:].rearrange("p (a k) -> p a k", k=D),
-                              in_=w.rearrange("(a p) k -> p a k", p=P))
-            wraw.append(wr)
         views = [v.rearrange("(p t) k -> p t k", t=NT) for v in (x, h_prev, c_prev)]
-        where = [[], [], []]
-        t0 = 0
-        for g, n in enumerate(LOAD_GROUPS):
-            for i in range(3):
-                rt = resid.tile([P, n * D], BF16, name="in%d_%d" % (i, g))
-                nc.sync.dma_start(out=rt[:].rearrange("p (t k) -> p t k", k=D),
-                                  in_=views[i][:, t0:t0 + n, :])
-                for j in range(n):
-                    where[i].append((rt, j))
-            t0 += n
         outs = [o.rearrange("(p t) n -> p t n", t=NT) for o in (out_0, out_1, out_2)]
+        where = [{}, {}, {}]
 
-        bias = const.tile([P, 2 * H], F32, name="bias")
-        lam = const.tile([P, H], F32, name="lam")
-        for half in range(3):
-            bp = apsum.tile([P, H], F32, name="bp%d" % half, tag="acc")
-            nc.tensor.matmul(out=bp[:], lhsT=ones[:], rhs=vecs[:, half * H:(half + 1) * H],
-                             start=True, stop=True)
-            if half < 2:
-                nc.vector.tensor_copy(out=bias[:, half * H:(half + 1) * H], in_=bp[:])
-            else:
-                nc.scalar.activation(out=lam[:], in_=bp[:], func=ACT.Exp)
+        def load(i, t0, n, tag):
+            rt = resid.tile([P, n * D], BF16, name="in%d_%d" % (i, t0), tag=tag)
+            nc.sync.dma_start(out=rt[:].rearrange("p (t k) -> p t k", k=D), in_=views[i][:, t0:t0 + n, :])
+            for j in range(n):
+                where[i][t0 + j] = (rt, j)
+
+        def load_w(op, half, tag):
+            w = (W_ih, W_hh)[op]
+            wr = stage.tile([P, 4 * D], BF16, name="wraw%d%d" % (op, half), tag=tag)
+            nc.sync.dma_start(out=wr[:].rearrange("p (a k) -> p a k", k=D),
+                              in_=w[half * H:(half + 1) * H, :].rearrange("(a p) k -> p a k", p=P))
+            return wr
+
+        load(0, 0, 4, "x0")
+        load(1, 0, 4, "h0")
+        wraw = {}
+        wraw[(0, 1)] = load_w(0, 1, "zst")
+        wraw[(1, 1)] = load_w(1, 1, "mst")
+        wraw[(0, 0)] = load_w(0, 0, "ist")
+        wraw[(1, 0)] = load_w(1, 0, "zst")
+        load(2, 0, 4, "c0")
+        load(0, 4, 4, "x4")
+        load(1, 4, 4, "h4")
+        load(2, 4, 4, "c4")
+        for t0 in (8, 16):
+            load(0, t0, 8, "x%d" % t0)
+            load(1, t0, 8, "h%d" % t0)
+            load(2, t0, 8, "c%d" % t0)
 
         wq = const.tile([P, 2, 2 * H], U32, name="wq", align_bytes=64)
         wsc = const.tile([P, 2, 2 * H], U8, name="wsc", align_bytes=64)
@@ -84,7 +87,7 @@ def tile_koslmcell_pa_t_kernel(tc, x, h_prev, c_prev, W_ih, b_ih, W_hh, b_hh,
         def transposes(srcs, label, engines):
             grouped = gpool.tile([P, 4 * P, 2], F32, name="grp_" + label, tag="grp", align_bytes=64)
             for half in range(2):
-                tp = tpsum.tile([P, 2, 2, P], F32, name="tp_%s_%d" % (label, half), tag="tp")
+                tp = ps.tile([P, 2, 2, P], F32, name="tp_%s_%d" % (label, half), tag="ps")
                 for a in range(2):
                     for u in range(2):
                         nc.tensor.transpose(tp[:, a, u, :], srcs[2 * half + a][:, u * P:(u + 1) * P], ident[:])
@@ -100,59 +103,116 @@ def tile_koslmcell_pa_t_kernel(tc, x, h_prev, c_prev, W_ih, b_ih, W_hh, b_hh,
             nc.vector.quantize_mx(out=codes.bitcast(FP8X4), scales=scales,
                                   in_=grouped[:].rearrange("p c u -> p (c u)").bitcast(BF16))
 
-        wg = []
-        for op in range(2):
-            wv = wraw[op][:].bitcast(F32)
-            for u in range(2):
-                srcs = [wv[:, (4 * u + a) * (D // 2):(4 * u + a + 1) * (D // 2)] for a in range(4)]
-                wg.append((transposes(srcs, "w%d%d" % (op, u), "sv"), op, u))
-        for g, op, u in wg:
-            quantise(g, wq[:, op, u * H:(u + 1) * H], wsc[:, op, u * H:(u + 1) * H])
+        def t1_w(op, half, engines):
+            wv = wraw[(op, half)][:].bitcast(F32)
+            srcs = [wv[:, a * (D // 2):(a + 1) * (D // 2)] for a in range(4)]
+            return transposes(srcs, "w%d%d" % (op, half), engines)
 
-        def prep(b):
-            gs = []
-            for op in range(2):
-                srcs = []
-                for t in range(b * TB, (b + 1) * TB):
-                    rt, j = where[op][t]
-                    srcs.append(rt[:].bitcast(F32)[:, j * (D // 2):(j + 1) * (D // 2)])
-                gs.append(transposes(srcs, "b%d_%d" % (b, op), "ss"))
-            res = []
-            for op in range(2):
-                q = qpool.tile([P, TB * P], U32, name="q%d_%d" % (b, op), tag="q%d" % op, align_bytes=64)
-                s = qpool.tile([P, TB * P], U8, name="s%d_%d" % (b, op), tag="s%d" % op, align_bytes=64)
-                quantise(gs[op], q[:], s[:])
-                res.append((q, s))
-            return res
+        def quant_w(g, op, half):
+            quantise(g, wq[:, op, half * H:(half + 1) * H], wsc[:, op, half * H:(half + 1) * H])
 
-        nxt = prep(0)
+        def t1_in(b, op, engines):
+            srcs = []
+            for t in range(b * TB, (b + 1) * TB):
+                rt, j = where[op][t]
+                srcs.append(rt[:].bitcast(F32)[:, j * (D // 2):(j + 1) * (D // 2)])
+            return transposes(srcs, "b%d_%d" % (b, op), engines)
+
+        def quant_in(g, b, op):
+            q = qpool.tile([P, TB * P], U32, name="q%d_%d" % (b, op), tag="q%d" % op, align_bytes=64)
+            s = qpool.tile([P, TB * P], U8, name="s%d_%d" % (b, op), tag="s%d" % op, align_bytes=64)
+            quantise(g, q[:], s[:])
+            return (q, s)
+
+        gx = t1_in(0, 0, "sv")
+        gh = t1_in(0, 1, "sv")
+        cur = [quant_in(gx, 0, 0)]
+        gw0 = t1_w(0, 1, "sv")
+        cur.append(quant_in(gh, 0, 1))
+        gw1 = t1_w(1, 1, "sv")
+        quant_w(gw0, 0, 1)
+
+        bias_z = const.tile([P, H], F32, name="bias_z")
+        bzp = ps.tile([P, H], F32, name="bzp", tag="ps")
+        nc.tensor.matmul(out=bzp[:], lhsT=ones[:], rhs=vecs[:, 0:H], start=True, stop=True)
+        nc.vector.tensor_copy(out=bias_z[:], in_=bzp[:])
+        pp = ps.tile([P, 8, 32], F32, name="pp", tag="ps")
+        for j in range(8):
+            nc.tensor.matmul(out=pp[:, j, :], lhsT=vecs[:, H + j * P:H + (j + 1) * P], rhs=ones[:, 0:32],
+                             start=True, stop=True)
+        bias_m = const.tile([P, 4], F32, name="bias_m")
+        nc.scalar.copy(out=bias_m[:], in_=pp[:, 0:4, 0])
+        lam = const.tile([P, 4], F32, name="lam")
+        nc.scalar.activation(out=lam[:], in_=pp[:, 4:8, 0], func=ACT.Exp)
+        lam15 = const.tile([P, 4], F32, name="lam15")
+        nc.vector.tensor_scalar_mul(out=lam15[:], in0=lam[:], scalar1=M_SCALE)
+        quant_w(gw1, 1, 1)
+
         for b in range(NB):
-            cur = nxt
+            tms, us = [], []
+            for j in range(4):
+                am = ps.tile([P, TB * P], F32, name="am%d_%d" % (b, j), tag="ps")
+                for op in range(2):
+                    q, s = cur[op]
+                    nc.tensor.matmul_mx(out=am[:],
+                                        lhsT=wq[:, op, H + j * P:H + (j + 1) * P].bitcast(FP8X4),
+                                        lhsT_scale=wsc[:, op, H + j * P:H + (j + 1) * P],
+                                        rhs=q[:].bitcast(FP8X4), rhs_scale=s[:],
+                                        start=(op == 0), stop=(op == 1))
+                tm = tpool.tile([P, TB * P], F32, name="tm%d_%d" % (b, j), tag="tm", bufs=6)
+                nc.scalar.activation(out=tm[:], in_=am[:], func=ACT.Tanh, bias=bias_m[:, j:j + 1])
+                u = tpool.tile([P, TB * P], F32, name="u%d_%d" % (b, j), tag="u", bufs=4)
+                nc.vector.tensor_scalar_mul(out=u[:], in0=tm[:], scalar1=lam15[:, j:j + 1])
+                tms.append(tm)
+                us.append(u)
+            if b == 0:
+                gw0 = t1_w(0, 0, "sv")
+                gw1 = t1_w(1, 0, "sv")
+                quant_w(gw0, 0, 0)
             if b + 1 < NB:
-                nxt = prep(b + 1)
+                gx = t1_in(b + 1, 0, "ss")
+                gh = t1_in(b + 1, 1, "ss")
+            if b == 0:
+                quant_w(gw1, 1, 0)
             zst = stage.tile([P, TB, H], F32, name="zst%d" % b, tag="zst")
             mst = stage.tile([P, TB, H], F32, name="mst%d" % b, tag="mst")
             ist = stage.tile([P, TB, H], F32, name="ist%d" % b, tag="ist")
-            for i in range(TB):
-                ct, j = where[2][b * TB + i]
-                nc.gpsimd.tensor_tensor(out=ist[:, i, :], in0=ct[:, j * H:(j + 1) * H], in1=lam[:], op=ALU.mult)
+            nxt = []
             for i in range(TB):
                 cols = slice(i * P, (i + 1) * P)
-                accs = [apsum.tile([P, H], F32, name="acc%d_%d_%d" % (b, i, half), tag="acc") for half in range(2)]
+                az = ps.tile([P, H], F32, name="az%d_%d" % (b, i), tag="ps")
                 for op in range(2):
                     q, s = cur[op]
-                    for half in range(2):
-                        nc.tensor.matmul_mx(out=accs[half][:],
-                                            lhsT=q[:, cols].bitcast(FP8X4), lhsT_scale=s[:, cols],
-                                            rhs=wq[:, op, half * H:(half + 1) * H].bitcast(FP8X4),
-                                            rhs_scale=wsc[:, op, half * H:(half + 1) * H],
-                                            start=(op == 0), stop=(op == 1))
-                nc.vector.tensor_tensor(out=zst[:, i, :], in0=accs[0][:], in1=bias[:, 0:H], op=ALU.add)
-                nc.vector.tensor_tensor(out=mst[:, i, :], in0=accs[1][:], in1=bias[:, H:2 * H], op=ALU.add)
+                    nc.tensor.matmul_mx(out=az[:],
+                                        lhsT=q[:, cols].bitcast(FP8X4), lhsT_scale=s[:, cols],
+                                        rhs=wq[:, op, 0:H].bitcast(FP8X4), rhs_scale=wsc[:, op, 0:H],
+                                        start=(op == 0), stop=(op == 1))
+                nc.vector.tensor_tensor(out=zst[:, i, :], in0=az[:], in1=bias_z[:], op=ALU.add)
                 nc.scalar.activation(out=zst[:, i, :], in_=zst[:, i, :], func=ACT.Tanh)
-                nc.scalar.activation(out=mst[:, i, :], in_=mst[:, i, :], func=ACT.Tanh)
-                nc.scalar.mul(out=mst[:, i, :], in_=mst[:, i, :], mul=M_SCALE)
-                nc.vector.tensor_tensor(out=ist[:, i, :], in0=ist[:, i, :], in1=mst[:, i, :], op=ALU.mult)
+                if b + 1 < NB and i == 0:
+                    nxt.append(quant_in(gx, b + 1, 0))
+                if b + 1 < NB and i == 1:
+                    nxt.append(quant_in(gh, b + 1, 1))
+            nc.sync.dma_start(out=outs[0][:, b * TB:(b + 1) * TB, :], in_=zst[:])
+            for i in range(TB):
+                cols = slice(i * P, (i + 1) * P)
+                tb = ps.tile([P, H], F32, name="tb%d_%d" % (b, i), tag="ps")
+                for j in range(4):
+                    nc.tensor.transpose(tb[:, j * P:(j + 1) * P], tms[j][:, cols], ident[:])
+                ub = ps.tile([P, H], F32, name="ub%d_%d" % (b, i), tag="ps")
+                for j in range(4):
+                    nc.tensor.transpose(ub[:, j * P:(j + 1) * P], us[j][:, cols], ident[:])
+                nc.scalar.mul(out=mst[:, i, :], in_=tb[:], mul=M_SCALE)
+                ct, j = where[2][b * TB + i]
+                nc.vector.tensor_tensor(out=ist[:, i, :], in0=ub[:], in1=ct[:, j * H:(j + 1) * H], op=ALU.mult)
                 nc.vector.tensor_tensor(out=ist[:, i, :], in0=ist[:, i, :], in1=zst[:, i, :], op=ALU.add)
-            for o, st in zip(outs, (zst, mst, ist)):
-                nc.sync.dma_start(out=o[:, b * TB:(b + 1) * TB, :], in_=st[:])
+            nc.sync.dma_start(out=outs[1][:, b * TB:(b + 1) * TB, :], in_=mst[:])
+            nc.sync.dma_start(out=outs[2][:, b * TB:(b + 1) * TB, :], in_=ist[:])
+            if b == 0:
+                load(0, 24, 4, "x0")
+                load(1, 24, 4, "h0")
+                load(2, 24, 8, "c24")
+            if b == 1:
+                load(0, 28, 4, "x4")
+                load(1, 28, 4, "h4")
+            cur = nxt

@@ -53,7 +53,7 @@ def tile_koslmcell_pa_t_kernel(tc, x, h_prev, c_prev, W_ih, b_ih, W_hh, b_hh,
         where = [{}, {}, {}]
 
         def load(i, t0, n, tag):
-            rt = resid.tile([P, n * D], BF16, name="in%d_%d" % (i, t0), tag=tag)
+            rt = resid.tile([P, n * D], BF16, name="in%d_%d" % (i, t0), tag="%s%d" % ("xhc"[i], tag))
             nc.sync.dma_start(out=rt[:].rearrange("p (t k) -> p t k", k=D), in_=views[i][:, t0:t0 + n, :])
             for j in range(n):
                 where[i][t0 + j] = (rt, j)
@@ -65,21 +65,23 @@ def tile_koslmcell_pa_t_kernel(tc, x, h_prev, c_prev, W_ih, b_ih, W_hh, b_hh,
                               in_=w[half * H:(half + 1) * H, :].rearrange("(a p) k -> p a k", p=P))
             return wr
 
-        load(0, 0, 4, "x0")
-        load(1, 0, 4, "h0")
+        load(0, 0, 4, 0)
+        load(1, 0, 4, 0)
         wraw = {}
         wraw[(0, 1)] = load_w(0, 1, "zst")
         wraw[(1, 1)] = load_w(1, 1, "mst")
         wraw[(0, 0)] = load_w(0, 0, "ist")
         wraw[(1, 0)] = load_w(1, 0, "zst")
-        load(2, 0, 4, "c0")
-        load(0, 4, 4, "x4")
-        load(1, 4, 4, "h4")
-        load(2, 4, 4, "c4")
-        for t0 in (8, 16):
-            load(0, t0, 8, "x%d" % t0)
-            load(1, t0, 8, "h%d" % t0)
-            load(2, t0, 8, "c%d" % t0)
+        for t0 in (4, 8):
+            load(0, t0, 4, t0)
+            load(1, t0, 4, t0)
+        load(2, 0, 4, 0)
+        load(0, 12, 4, 12)
+        load(1, 12, 4, 12)
+        load(2, 4, 4, 4)
+        load(0, 16, 8, 16)
+        load(1, 16, 8, 16)
+        load(2, 8, 8, 8)
 
         wq = const.tile([P, 2, 2 * H], U32, name="wq", align_bytes=64)
         wsc = const.tile([P, 2, 2 * H], U8, name="wsc", align_bytes=64)
@@ -103,34 +105,37 @@ def tile_koslmcell_pa_t_kernel(tc, x, h_prev, c_prev, W_ih, b_ih, W_hh, b_hh,
             nc.vector.quantize_mx(out=codes.bitcast(FP8X4), scales=scales,
                                   in_=grouped[:].rearrange("p c u -> p (c u)").bitcast(BF16))
 
-        def t1_w(op, half, engines):
+        def t1_w(op, half):
             wv = wraw[(op, half)][:].bitcast(F32)
             srcs = [wv[:, a * (D // 2):(a + 1) * (D // 2)] for a in range(4)]
-            return transposes(srcs, "w%d%d" % (op, half), engines)
+            return transposes(srcs, "w%d%d" % (op, half), "sv")
 
         def quant_w(g, op, half):
             quantise(g, wq[:, op, half * H:(half + 1) * H], wsc[:, op, half * H:(half + 1) * H])
 
-        def t1_in(b, op, engines):
+        def t1_in(b, op):
             srcs = []
             for t in range(b * TB, (b + 1) * TB):
                 rt, j = where[op][t]
                 srcs.append(rt[:].bitcast(F32)[:, j * (D // 2):(j + 1) * (D // 2)])
-            return transposes(srcs, "b%d_%d" % (b, op), engines)
+            return (transposes(srcs, "b%d_%d" % (b, op), "sv"), b, op)
 
-        def quant_in(g, b, op):
+        qs = {}
+
+        def quant_in(gbo):
+            g, b, op = gbo
             q = qpool.tile([P, TB * P], U32, name="q%d_%d" % (b, op), tag="q%d" % op, align_bytes=64)
             s = qpool.tile([P, TB * P], U8, name="s%d_%d" % (b, op), tag="s%d" % op, align_bytes=64)
             quantise(g, q[:], s[:])
-            return (q, s)
+            qs[(b, op)] = (q, s)
 
-        gx = t1_in(0, 0, "sv")
-        gh = t1_in(0, 1, "sv")
-        cur = [quant_in(gx, 0, 0)]
-        gw0 = t1_w(0, 1, "sv")
-        cur.append(quant_in(gh, 0, 1))
-        gw1 = t1_w(1, 1, "sv")
-        quant_w(gw0, 0, 1)
+        gx = t1_in(0, 0)
+        gh = t1_in(0, 1)
+        quant_in(gx)
+        gwm0 = t1_w(0, 1)
+        quant_in(gh)
+        gwm1 = t1_w(1, 1)
+        quant_w(gwm0, 0, 1)
 
         bias_z = const.tile([P, H], F32, name="bias_z")
         bzp = ps.tile([P, H], F32, name="bzp", tag="ps")
@@ -146,14 +151,16 @@ def tile_koslmcell_pa_t_kernel(tc, x, h_prev, c_prev, W_ih, b_ih, W_hh, b_hh,
         nc.scalar.activation(out=lam[:], in_=pp[:, 4:8, 0], func=ACT.Exp)
         lam15 = const.tile([P, 4], F32, name="lam15")
         nc.vector.tensor_scalar_mul(out=lam15[:], in0=lam[:], scalar1=M_SCALE)
-        quant_w(gw1, 1, 1)
+        gwz0 = t1_w(0, 0)
+        quant_w(gwm1, 1, 1)
 
         for b in range(NB):
+            last = b == NB - 1
             tms, us = [], []
             for j in range(4):
                 am = ps.tile([P, TB * P], F32, name="am%d_%d" % (b, j), tag="ps")
                 for op in range(2):
-                    q, s = cur[op]
+                    q, s = qs[(b, op)]
                     nc.tensor.matmul_mx(out=am[:],
                                         lhsT=wq[:, op, H + j * P:H + (j + 1) * P].bitcast(FP8X4),
                                         lhsT_scale=wsc[:, op, H + j * P:H + (j + 1) * P],
@@ -162,38 +169,35 @@ def tile_koslmcell_pa_t_kernel(tc, x, h_prev, c_prev, W_ih, b_ih, W_hh, b_hh,
                 tm = tpool.tile([P, TB * P], F32, name="tm%d_%d" % (b, j), tag="tm", bufs=6)
                 nc.scalar.activation(out=tm[:], in_=am[:], func=ACT.Tanh, bias=bias_m[:, j:j + 1])
                 u = tpool.tile([P, TB * P], F32, name="u%d_%d" % (b, j), tag="u", bufs=4)
-                nc.vector.tensor_scalar_mul(out=u[:], in0=tm[:], scalar1=lam15[:, j:j + 1])
+                nc.gpsimd.tensor_scalar(out=u[:], in0=tm[:], scalar1=lam15[:, j:j + 1], scalar2=0.0,
+                                        op0=ALU.mult, op1=ALU.add)
                 tms.append(tm)
                 us.append(u)
+            pend = []
             if b == 0:
-                gw0 = t1_w(0, 0, "sv")
-                gw1 = t1_w(1, 0, "sv")
-                quant_w(gw0, 0, 0)
-            if b + 1 < NB:
-                gx = t1_in(b + 1, 0, "ss")
-                gh = t1_in(b + 1, 1, "ss")
-            if b == 0:
-                quant_w(gw1, 1, 0)
+                gwz1 = t1_w(1, 0)
+                quant_w(gwz0, 0, 0)
+                pend.append(t1_in(1, 0))
+                pend.append(t1_in(1, 1))
+                quant_w(gwz1, 1, 0)
             zst = stage.tile([P, TB, H], F32, name="zst%d" % b, tag="zst")
             mst = stage.tile([P, TB, H], F32, name="mst%d" % b, tag="mst")
             ist = stage.tile([P, TB, H], F32, name="ist%d" % b, tag="ist")
-            nxt = []
             for i in range(TB):
                 cols = slice(i * P, (i + 1) * P)
                 az = ps.tile([P, H], F32, name="az%d_%d" % (b, i), tag="ps")
                 for op in range(2):
-                    q, s = cur[op]
+                    q, s = qs[(b, op)]
                     nc.tensor.matmul_mx(out=az[:],
                                         lhsT=q[:, cols].bitcast(FP8X4), lhsT_scale=s[:, cols],
                                         rhs=wq[:, op, 0:H].bitcast(FP8X4), rhs_scale=wsc[:, op, 0:H],
                                         start=(op == 0), stop=(op == 1))
                 nc.vector.tensor_tensor(out=zst[:, i, :], in0=az[:], in1=bias_z[:], op=ALU.add)
                 nc.scalar.activation(out=zst[:, i, :], in_=zst[:, i, :], func=ACT.Tanh)
-                if b + 1 < NB and i == 0:
-                    nxt.append(quant_in(gx, b + 1, 0))
-                if b + 1 < NB and i == 1:
-                    nxt.append(quant_in(gh, b + 1, 1))
             nc.sync.dma_start(out=outs[0][:, b * TB:(b + 1) * TB, :], in_=zst[:])
+            if b + 2 < NB:
+                pend.append(t1_in(b + 2, 0))
+                pend.append(t1_in(b + 2, 1))
             for i in range(TB):
                 cols = slice(i * P, (i + 1) * P)
                 tb = ps.tile([P, H], F32, name="tb%d_%d" % (b, i), tag="ps")
@@ -205,14 +209,23 @@ def tile_koslmcell_pa_t_kernel(tc, x, h_prev, c_prev, W_ih, b_ih, W_hh, b_hh,
                 nc.scalar.mul(out=mst[:, i, :], in_=tb[:], mul=M_SCALE)
                 ct, j = where[2][b * TB + i]
                 nc.vector.tensor_tensor(out=ist[:, i, :], in0=ub[:], in1=ct[:, j * H:(j + 1) * H], op=ALU.mult)
-                nc.vector.tensor_tensor(out=ist[:, i, :], in0=ist[:, i, :], in1=zst[:, i, :], op=ALU.add)
+                if i < len(pend):
+                    quant_in(pend[i])
+                if not (last and i >= 2):
+                    nc.gpsimd.tensor_tensor(out=ist[:, i, :], in0=ist[:, i, :], in1=zst[:, i, :], op=ALU.add)
             nc.sync.dma_start(out=outs[1][:, b * TB:(b + 1) * TB, :], in_=mst[:])
-            nc.sync.dma_start(out=outs[2][:, b * TB:(b + 1) * TB, :], in_=ist[:])
+            if last:
+                nc.sync.dma_start(out=outs[2][:, b * TB:b * TB + 2, :], in_=ist[:, 0:2, :])
+                for i in (2, 3):
+                    nc.vector.tensor_tensor(out=ist[:, i, :], in0=ist[:, i, :], in1=zst[:, i, :], op=ALU.add)
+                nc.sync.dma_start(out=outs[2][:, b * TB + 2:b * TB + 4, :], in_=ist[:, 2:4, :])
+            else:
+                nc.sync.dma_start(out=outs[2][:, b * TB:(b + 1) * TB, :], in_=ist[:])
             if b == 0:
-                load(0, 24, 4, "x0")
-                load(1, 24, 4, "h0")
-                load(2, 24, 8, "c24")
+                load(2, 16, 8, 16)
+                load(0, 24, 4, 0)
+                load(1, 24, 4, 0)
             if b == 1:
-                load(0, 28, 4, "x4")
-                load(1, 28, 4, "h4")
-            cur = nxt
+                load(2, 24, 8, 24)
+                load(0, 28, 4, 4)
+                load(1, 28, 4, 4)

@@ -28,7 +28,7 @@ def tile_koslmcell_pa_t_kernel(tc, x, h_prev, c_prev, W_ih, b_ih, W_hh, b_hh,
         resid = ctx.enter_context(tc.tile_pool(name="resid", bufs=1))
         gpool = ctx.enter_context(tc.tile_pool(name="gpool", bufs=4))
         qpool = ctx.enter_context(tc.tile_pool(name="qpool", bufs=3))
-        tpool = ctx.enter_context(tc.tile_pool(name="tpool", bufs=4))
+        tpool = ctx.enter_context(tc.tile_pool(name="tpool", bufs=8))
         stage = ctx.enter_context(tc.tile_pool(name="stage", bufs=3))
         ps = ctx.enter_context(tc.psum_pool(name="ps", bufs=8))
         ctx.enter_context(tc.manual_schedule())
@@ -69,9 +69,9 @@ def tile_koslmcell_pa_t_kernel(tc, x, h_prev, c_prev, W_ih, b_ih, W_hh, b_hh,
         load(1, 0, 4, 0)
         wraw = {}
         wraw[(0, 1)] = load_w(0, 1, "zst")
-        wraw[(1, 1)] = load_w(1, 1, "mst")
-        wraw[(0, 0)] = load_w(0, 0, "ist")
-        wraw[(1, 0)] = load_w(1, 0, "zst")
+        wraw[(1, 1)] = load_w(1, 1, "ist")
+        wraw[(0, 0)] = load_w(0, 0, "zst")
+        wraw[(1, 0)] = load_w(1, 0, "ist")
         for t0 in (4, 8):
             load(0, t0, 4, t0)
             load(1, t0, 4, t0)
@@ -82,6 +82,7 @@ def tile_koslmcell_pa_t_kernel(tc, x, h_prev, c_prev, W_ih, b_ih, W_hh, b_hh,
         load(0, 16, 8, 16)
         load(1, 16, 8, 16)
         load(2, 8, 8, 8)
+        load(2, 16, 8, 16)
 
         wq = const.tile([P, 2, 2 * H], U32, name="wq", align_bytes=64)
         wsc = const.tile([P, 2, 2 * H], U8, name="wsc", align_bytes=64)
@@ -113,12 +114,12 @@ def tile_koslmcell_pa_t_kernel(tc, x, h_prev, c_prev, W_ih, b_ih, W_hh, b_hh,
         def quant_w(g, op, half):
             quantise(g, wq[:, op, half * H:(half + 1) * H], wsc[:, op, half * H:(half + 1) * H])
 
-        def t1_in(b, op):
+        def t1_in(b, op, engines):
             srcs = []
             for t in range(b * TB, (b + 1) * TB):
                 rt, j = where[op][t]
                 srcs.append(rt[:].bitcast(F32)[:, j * (D // 2):(j + 1) * (D // 2)])
-            return (transposes(srcs, "b%d_%d" % (b, op), "sv"), b, op)
+            return (transposes(srcs, "b%d_%d" % (b, op), engines), b, op)
 
         qs = {}
 
@@ -129,8 +130,33 @@ def tile_koslmcell_pa_t_kernel(tc, x, h_prev, c_prev, W_ih, b_ih, W_hh, b_hh,
             quantise(g, q[:], s[:])
             qs[(b, op)] = (q, s)
 
-        gx = t1_in(0, 0)
-        gh = t1_in(0, 1)
+        tms = {}
+        msts = {}
+
+        def scaled_c(b):
+            mst = stage.tile([P, TB, H], F32, name="mst%d" % b, tag="mst")
+            msts[b] = mst
+            for i in range(TB):
+                ct, j = where[2][b * TB + i]
+                nc.gpsimd.tensor_tensor(out=mst[:, i, :], in0=ct[:, j * H:(j + 1) * H], in1=lam15[:], op=ALU.mult)
+
+        def mx_m(b):
+            tms[b] = []
+            for j in range(4):
+                am = ps.tile([P, TB * P], F32, name="am%d_%d" % (b, j), tag="ps")
+                for op in range(2):
+                    q, s = qs[(b, op)]
+                    nc.tensor.matmul_mx(out=am[:],
+                                        lhsT=wq[:, op, H + j * P:H + (j + 1) * P].bitcast(FP8X4),
+                                        lhsT_scale=wsc[:, op, H + j * P:H + (j + 1) * P],
+                                        rhs=q[:].bitcast(FP8X4), rhs_scale=s[:],
+                                        start=(op == 0), stop=(op == 1))
+                tm = tpool.tile([P, TB * P], F32, name="tm%d_%d" % (b, j), tag="tm")
+                nc.scalar.activation(out=tm[:], in_=am[:], func=ACT.Tanh, bias=bias_m[:, j:j + 1])
+                tms[b].append(tm)
+
+        gx = t1_in(0, 0, "sv")
+        gh = t1_in(0, 1, "sv")
         quant_in(gx)
         gwm0 = t1_w(0, 1)
         quant_in(gh)
@@ -141,48 +167,48 @@ def tile_koslmcell_pa_t_kernel(tc, x, h_prev, c_prev, W_ih, b_ih, W_hh, b_hh,
         bzp = ps.tile([P, H], F32, name="bzp", tag="ps")
         nc.tensor.matmul(out=bzp[:], lhsT=ones[:], rhs=vecs[:, 0:H], start=True, stop=True)
         nc.vector.tensor_copy(out=bias_z[:], in_=bzp[:])
-        pp = ps.tile([P, 8, 32], F32, name="pp", tag="ps")
-        for j in range(8):
+        lmp = ps.tile([P, H], F32, name="lmp", tag="ps")
+        nc.tensor.matmul(out=lmp[:], lhsT=ones[:], rhs=vecs[:, 2 * H:3 * H], start=True, stop=True)
+        lam = const.tile([P, H], F32, name="lam")
+        nc.scalar.activation(out=lam[:], in_=lmp[:], func=ACT.Exp)
+        lam15 = const.tile([P, H], F32, name="lam15")
+        nc.gpsimd.tensor_scalar(out=lam15[:], in0=lam[:], scalar1=M_SCALE, scalar2=0.0, op0=ALU.mult, op1=ALU.add)
+        pp = ps.tile([P, 4, 32], F32, name="pp", tag="ps")
+        for j in range(4):
             nc.tensor.matmul(out=pp[:, j, :], lhsT=vecs[:, H + j * P:H + (j + 1) * P], rhs=ones[:, 0:32],
                              start=True, stop=True)
         bias_m = const.tile([P, 4], F32, name="bias_m")
-        nc.scalar.copy(out=bias_m[:], in_=pp[:, 0:4, 0])
-        lam = const.tile([P, 4], F32, name="lam")
-        nc.scalar.activation(out=lam[:], in_=pp[:, 4:8, 0], func=ACT.Exp)
-        lam15 = const.tile([P, 4], F32, name="lam15")
-        nc.vector.tensor_scalar_mul(out=lam15[:], in0=lam[:], scalar1=M_SCALE)
+        nc.scalar.copy(out=bias_m[:], in_=pp[:, :, 0])
         gwz0 = t1_w(0, 0)
         quant_w(gwm1, 1, 1)
+        scaled_c(0)
+        mx_m(0)
+        gwz1 = t1_w(1, 0)
+        quant_w(gwz0, 0, 0)
+        gx = t1_in(1, 0, "sv")
+        gh = t1_in(1, 1, "sv")
+        quant_w(gwz1, 1, 0)
+        quant_in(gx)
+        quant_in(gh)
+        load(0, 24, 4, 0)
+        load(1, 24, 4, 0)
+        load(2, 24, 8, 24)
+        load(0, 28, 4, 4)
+        load(1, 28, 4, 4)
+        waiting = {2: (t1_in(2, 0, "sv"), t1_in(2, 1, "sv"))}
+
+        zsts = {}
+        ists = {}
+
+        def final_add(b, lo, hi):
+            nc.vector.tensor_tensor(out=ists[b][:, lo:hi, :], in0=ists[b][:, lo:hi, :], in1=zsts[b][:, lo:hi, :],
+                                    op=ALU.add)
 
         for b in range(NB):
-            last = b == NB - 1
-            tms, us = [], []
-            for j in range(4):
-                am = ps.tile([P, TB * P], F32, name="am%d_%d" % (b, j), tag="ps")
-                for op in range(2):
-                    q, s = qs[(b, op)]
-                    nc.tensor.matmul_mx(out=am[:],
-                                        lhsT=wq[:, op, H + j * P:H + (j + 1) * P].bitcast(FP8X4),
-                                        lhsT_scale=wsc[:, op, H + j * P:H + (j + 1) * P],
-                                        rhs=q[:].bitcast(FP8X4), rhs_scale=s[:],
-                                        start=(op == 0), stop=(op == 1))
-                tm = tpool.tile([P, TB * P], F32, name="tm%d_%d" % (b, j), tag="tm", bufs=6)
-                nc.scalar.activation(out=tm[:], in_=am[:], func=ACT.Tanh, bias=bias_m[:, j:j + 1])
-                u = tpool.tile([P, TB * P], F32, name="u%d_%d" % (b, j), tag="u", bufs=4)
-                nc.gpsimd.tensor_scalar(out=u[:], in0=tm[:], scalar1=lam15[:, j:j + 1], scalar2=0.0,
-                                        op0=ALU.mult, op1=ALU.add)
-                tms.append(tm)
-                us.append(u)
-            pend = []
-            if b == 0:
-                gwz1 = t1_w(1, 0)
-                quant_w(gwz0, 0, 0)
-                pend.append(t1_in(1, 0))
-                pend.append(t1_in(1, 1))
-                quant_w(gwz1, 1, 0)
             zst = stage.tile([P, TB, H], F32, name="zst%d" % b, tag="zst")
-            mst = stage.tile([P, TB, H], F32, name="mst%d" % b, tag="mst")
             ist = stage.tile([P, TB, H], F32, name="ist%d" % b, tag="ist")
+            zsts[b] = zst
+            ists[b] = ist
             for i in range(TB):
                 cols = slice(i * P, (i + 1) * P)
                 az = ps.tile([P, H], F32, name="az%d_%d" % (b, i), tag="ps")
@@ -195,37 +221,28 @@ def tile_koslmcell_pa_t_kernel(tc, x, h_prev, c_prev, W_ih, b_ih, W_hh, b_hh,
                 nc.vector.tensor_tensor(out=zst[:, i, :], in0=az[:], in1=bias_z[:], op=ALU.add)
                 nc.scalar.activation(out=zst[:, i, :], in_=zst[:, i, :], func=ACT.Tanh)
             nc.sync.dma_start(out=outs[0][:, b * TB:(b + 1) * TB, :], in_=zst[:])
+            if b > 0:
+                final_add(b - 1, 0, 2)
+                final_add(b - 1, 2, 4)
+                nc.sync.dma_start(out=outs[2][:, (b - 1) * TB:b * TB, :], in_=ists[b - 1][:])
             if b + 2 < NB:
-                pend.append(t1_in(b + 2, 0))
-                pend.append(t1_in(b + 2, 1))
+                quant_in(waiting[b + 2][0])
+                quant_in(waiting[b + 2][1])
+            if b + 1 < NB:
+                scaled_c(b + 1)
+                mx_m(b + 1)
+            if b + 3 < NB:
+                waiting[b + 3] = (t1_in(b + 3, 0, "ss"), t1_in(b + 3, 1, "sv"))
+            mst = msts[b]
             for i in range(TB):
                 cols = slice(i * P, (i + 1) * P)
                 tb = ps.tile([P, H], F32, name="tb%d_%d" % (b, i), tag="ps")
                 for j in range(4):
-                    nc.tensor.transpose(tb[:, j * P:(j + 1) * P], tms[j][:, cols], ident[:])
-                ub = ps.tile([P, H], F32, name="ub%d_%d" % (b, i), tag="ps")
-                for j in range(4):
-                    nc.tensor.transpose(ub[:, j * P:(j + 1) * P], us[j][:, cols], ident[:])
+                    nc.tensor.transpose(tb[:, j * P:(j + 1) * P], tms[b][j][:, cols], ident[:])
+                nc.vector.tensor_tensor(out=ist[:, i, :], in0=tb[:], in1=mst[:, i, :], op=ALU.mult)
                 nc.scalar.mul(out=mst[:, i, :], in_=tb[:], mul=M_SCALE)
-                ct, j = where[2][b * TB + i]
-                nc.vector.tensor_tensor(out=ist[:, i, :], in0=ub[:], in1=ct[:, j * H:(j + 1) * H], op=ALU.mult)
-                if i < len(pend):
-                    quant_in(pend[i])
-                if not (last and i >= 2):
-                    nc.gpsimd.tensor_tensor(out=ist[:, i, :], in0=ist[:, i, :], in1=zst[:, i, :], op=ALU.add)
             nc.sync.dma_start(out=outs[1][:, b * TB:(b + 1) * TB, :], in_=mst[:])
-            if last:
-                nc.sync.dma_start(out=outs[2][:, b * TB:b * TB + 2, :], in_=ist[:, 0:2, :])
-                for i in (2, 3):
-                    nc.vector.tensor_tensor(out=ist[:, i, :], in0=ist[:, i, :], in1=zst[:, i, :], op=ALU.add)
-                nc.sync.dma_start(out=outs[2][:, b * TB + 2:b * TB + 4, :], in_=ist[:, 2:4, :])
-            else:
-                nc.sync.dma_start(out=outs[2][:, b * TB:(b + 1) * TB, :], in_=ist[:])
-            if b == 0:
-                load(2, 16, 8, 16)
-                load(0, 24, 4, 0)
-                load(1, 24, 4, 0)
-            if b == 1:
-                load(2, 24, 8, 24)
-                load(0, 28, 4, 4)
-                load(1, 28, 4, 4)
+        b = NB - 1
+        for lo in (0, 2):
+            final_add(b, lo, lo + 2)
+            nc.sync.dma_start(out=outs[2][:, b * TB + lo:b * TB + lo + 2, :], in_=ists[b][:, lo:lo + 2, :])

@@ -72,13 +72,14 @@ def tile_koslmcell_pa_t_kernel(tc, x, h_prev, c_prev, W_ih, b_ih, W_hh, b_hh,
         wraw[(1, 1)] = load_w(1, 1, "ist")
         wraw[(0, 0)] = load_w(0, 0, "zst")
         wraw[(1, 0)] = load_w(1, 0, "ist")
-        for t0 in (4, 8):
-            load(0, t0, 4, t0)
-            load(1, t0, 4, t0)
+        load(0, 4, 4, 4)
+        load(1, 4, 4, 4)
         load(2, 0, 4, 0)
+        load(0, 8, 4, 8)
+        load(1, 8, 4, 8)
+        load(2, 4, 4, 4)
         load(0, 12, 4, 12)
         load(1, 12, 4, 12)
-        load(2, 4, 4, 4)
         load(0, 16, 8, 16)
         load(1, 16, 8, 16)
         load(2, 8, 8, 8)
@@ -181,21 +182,8 @@ def tile_koslmcell_pa_t_kernel(tc, x, h_prev, c_prev, W_ih, b_ih, W_hh, b_hh,
         nc.scalar.copy(out=bias_m[:], in_=pp[:, :, 0])
         gwz0 = t1_w(0, 0)
         quant_w(gwm1, 1, 1)
-        scaled_c(0)
-        mx_m(0)
         gwz1 = t1_w(1, 0)
         quant_w(gwz0, 0, 0)
-        gx = t1_in(1, 0, "sv")
-        gh = t1_in(1, 1, "sv")
-        quant_w(gwz1, 1, 0)
-        quant_in(gx)
-        quant_in(gh)
-        load(0, 24, 4, 0)
-        load(1, 24, 4, 0)
-        load(2, 24, 8, 24)
-        load(0, 28, 4, 4)
-        load(1, 28, 4, 4)
-        waiting = {2: (t1_in(2, 0, "sv"), t1_in(2, 1, "sv"))}
 
         zsts = {}
         ists = {}
@@ -204,45 +192,55 @@ def tile_koslmcell_pa_t_kernel(tc, x, h_prev, c_prev, W_ih, b_ih, W_hh, b_hh,
             nc.vector.tensor_tensor(out=ists[b][:, lo:hi, :], in0=ists[b][:, lo:hi, :], in1=zsts[b][:, lo:hi, :],
                                     op=ALU.add)
 
-        for b in range(NB):
-            zst = stage.tile([P, TB, H], F32, name="zst%d" % b, tag="zst")
-            ist = stage.tile([P, TB, H], F32, name="ist%d" % b, tag="ist")
-            zsts[b] = zst
-            ists[b] = ist
-            for i in range(TB):
-                cols = slice(i * P, (i + 1) * P)
-                az = ps.tile([P, H], F32, name="az%d_%d" % (b, i), tag="ps")
-                for op in range(2):
-                    q, s = qs[(b, op)]
-                    nc.tensor.matmul_mx(out=az[:],
-                                        lhsT=q[:, cols].bitcast(FP8X4), lhsT_scale=s[:, cols],
-                                        rhs=wq[:, op, 0:H].bitcast(FP8X4), rhs_scale=wsc[:, op, 0:H],
-                                        start=(op == 0), stop=(op == 1))
-                nc.vector.tensor_tensor(out=zst[:, i, :], in0=az[:], in1=bias_z[:], op=ALU.add)
-                nc.scalar.activation(out=zst[:, i, :], in_=zst[:, i, :], func=ACT.Tanh)
-            nc.sync.dma_start(out=outs[0][:, b * TB:(b + 1) * TB, :], in_=zst[:])
-            if b > 0:
-                final_add(b - 1, 0, 2)
-                final_add(b - 1, 2, 4)
-                nc.sync.dma_start(out=outs[2][:, (b - 1) * TB:b * TB, :], in_=ists[b - 1][:])
-            if b + 2 < NB:
-                quant_in(waiting[b + 2][0])
-                quant_in(waiting[b + 2][1])
+        for b in range(NB + 1):
+            c = b - 1
+            fresh = ()
             if b + 1 < NB:
-                scaled_c(b + 1)
-                mx_m(b + 1)
-            if b + 3 < NB:
-                waiting[b + 3] = (t1_in(b + 3, 0, "ss"), t1_in(b + 3, 1, "sv"))
-            mst = msts[b]
-            for i in range(TB):
-                cols = slice(i * P, (i + 1) * P)
-                tb = ps.tile([P, H], F32, name="tb%d_%d" % (b, i), tag="ps")
-                for j in range(4):
-                    nc.tensor.transpose(tb[:, j * P:(j + 1) * P], tms[b][j][:, cols], ident[:])
-                nc.vector.tensor_tensor(out=ist[:, i, :], in0=tb[:], in1=mst[:, i, :], op=ALU.mult)
-                nc.scalar.mul(out=mst[:, i, :], in_=tb[:], mul=M_SCALE)
-            nc.sync.dma_start(out=outs[1][:, b * TB:(b + 1) * TB, :], in_=mst[:])
-        b = NB - 1
-        for lo in (0, 2):
-            final_add(b, lo, lo + 2)
-            nc.sync.dma_start(out=outs[2][:, b * TB + lo:b * TB + lo + 2, :], in_=ists[b][:, lo:lo + 2, :])
+                how = "sv" if b == 0 else "ss"
+                fresh = (t1_in(b + 1, 0, how), t1_in(b + 1, 1, how))
+            if b == 0:
+                quant_w(gwz1, 1, 0)
+                load(0, 24, 4, 0)
+                load(1, 24, 4, 0)
+                load(2, 24, 8, 24)
+                load(0, 28, 4, 4)
+                load(1, 28, 4, 4)
+            if c >= 0:
+                ist = stage.tile([P, TB, H], F32, name="ist%d" % c, tag="ist")
+                ists[c] = ist
+                mst = msts[c]
+                for i in range(TB):
+                    cols = slice(i * P, (i + 1) * P)
+                    tb = ps.tile([P, H], F32, name="tb%d_%d" % (c, i), tag="ps")
+                    for j in range(4):
+                        nc.tensor.transpose(tb[:, j * P:(j + 1) * P], tms[c][j][:, cols], ident[:])
+                    nc.vector.tensor_tensor(out=ist[:, i, :], in0=tb[:], in1=mst[:, i, :], op=ALU.mult)
+                    nc.scalar.mul(out=mst[:, i, :], in_=tb[:], mul=M_SCALE)
+                nc.sync.dma_start(out=outs[1][:, c * TB:(c + 1) * TB, :], in_=mst[:])
+                if b < NB:
+                    final_add(c, 0, 2)
+                    final_add(c, 2, 4)
+                    nc.sync.dma_start(out=outs[2][:, c * TB:(c + 1) * TB, :], in_=ist[:])
+                else:
+                    for lo in (0, 2):
+                        final_add(c, lo, lo + 2)
+                        nc.sync.dma_start(out=outs[2][:, c * TB + lo:c * TB + lo + 2, :], in_=ist[:, lo:lo + 2, :])
+            for g in fresh:
+                quant_in(g)
+            if b < NB:
+                scaled_c(b)
+                mx_m(b)
+                zst = stage.tile([P, TB, H], F32, name="zst%d" % b, tag="zst")
+                zsts[b] = zst
+                for i in range(TB):
+                    cols = slice(i * P, (i + 1) * P)
+                    az = ps.tile([P, H], F32, name="az%d_%d" % (b, i), tag="ps")
+                    for op in range(2):
+                        q, s = qs[(b, op)]
+                        nc.tensor.matmul_mx(out=az[:],
+                                            lhsT=q[:, cols].bitcast(FP8X4), lhsT_scale=s[:, cols],
+                                            rhs=wq[:, op, 0:H].bitcast(FP8X4), rhs_scale=wsc[:, op, 0:H],
+                                            start=(op == 0), stop=(op == 1))
+                    nc.vector.tensor_tensor(out=zst[:, i, :], in0=az[:], in1=bias_z[:], op=ALU.add)
+                    nc.scalar.activation(out=zst[:, i, :], in_=zst[:, i, :], func=ACT.Tanh)
+                nc.sync.dma_start(out=outs[0][:, b * TB:(b + 1) * TB, :], in_=zst[:])

@@ -14,6 +14,7 @@ ALU = mybir.AluOpType
 P = 128
 B, D, H = 4096, 512, 512
 NT = B // P
+TG = 8
 TB = 4
 NB = NT // TB
 M_SCALE = 1.5
@@ -48,21 +49,23 @@ def tile_koslmcell_pa_t_kernel(tc, x, h_prev, c_prev, W_ih, b_ih, W_hh, b_hh,
         ident = const.tile([P, P], F32, name="ident")
         make_identity(nc, ident[:])
 
-        views = [v.rearrange("(p t) k -> p t k", t=NT) for v in (x, h_prev, c_prev)]
-        outs = [o.rearrange("(p t) n -> p t n", t=NT) for o in (out_0, out_1, out_2)]
+        views = [v.rearrange("(g p t) k -> g p t k", p=P, t=TG) for v in (x, h_prev, c_prev)]
+        outs = [o.rearrange("(g p t) n -> g p t n", p=P, t=TG) for o in (out_0, out_1, out_2)]
+
+        def dram(view, t0, n):
+            return view[t0 // TG, :, t0 % TG:t0 % TG + n, :]
         where = [{}, {}, {}]
 
         def load(i, t0, n, tag):
             rt = resid.tile([P, n * D], BF16, name="in%d_%d" % (i, t0), tag="%s%d" % ("xhc"[i], tag))
-            nc.sync.dma_start(out=rt[:].rearrange("p (t k) -> p t k", k=D), in_=views[i][:, t0:t0 + n, :])
+            nc.sync.dma_start(out=rt[:].rearrange("p (t k) -> p t k", k=D), in_=dram(views[i], t0, n))
             for j in range(n):
                 where[i][t0 + j] = (rt, j)
 
         def load_w(op, half, tag):
             w = (W_ih, W_hh)[op]
             wr = stage.tile([P, 4 * D], BF16, name="wraw%d%d" % (op, half), tag=tag)
-            nc.sync.dma_start(out=wr[:].rearrange("p (a k) -> p a k", k=D),
-                              in_=w[half * H:(half + 1) * H, :].rearrange("(a p) k -> p a k", p=P))
+            nc.sync.dma_start(out=wr[:], in_=w[half * H:(half + 1) * H, :].rearrange("(p a) k -> p (a k)", a=4))
             return wr
 
         load(0, 0, 4, 0)
@@ -75,11 +78,9 @@ def tile_koslmcell_pa_t_kernel(tc, x, h_prev, c_prev, W_ih, b_ih, W_hh, b_hh,
         load(0, 4, 4, 4)
         load(1, 4, 4, 4)
         load(2, 0, 4, 0)
-        load(0, 8, 4, 8)
-        load(1, 8, 4, 8)
+        load(0, 8, 8, 8)
+        load(1, 8, 8, 8)
         load(2, 4, 4, 4)
-        load(0, 12, 4, 12)
-        load(1, 12, 4, 12)
         load(0, 16, 8, 16)
         load(1, 16, 8, 16)
         load(2, 8, 8, 8)
@@ -88,15 +89,19 @@ def tile_koslmcell_pa_t_kernel(tc, x, h_prev, c_prev, W_ih, b_ih, W_hh, b_hh,
         wq = const.tile([P, 2, 2 * H], U32, name="wq", align_bytes=64)
         wsc = const.tile([P, 2, 2 * H], U8, name="wsc", align_bytes=64)
 
-        def transposes(srcs, label, engines):
+        def transposes(srcs, label, engines, rows_interleaved=False):
             grouped = gpool.tile([P, 4 * P, 2], F32, name="grp_" + label, tag="grp", align_bytes=64)
             for half in range(2):
                 tp = ps.tile([P, 2, 2, P], F32, name="tp_%s_%d" % (label, half), tag="ps")
                 for a in range(2):
                     for u in range(2):
                         nc.tensor.transpose(tp[:, a, u, :], srcs[2 * half + a][:, u * P:(u + 1) * P], ident[:])
-                dst = grouped[:, 2 * P * half:2 * P * (half + 1), :].rearrange("p (a r) u -> p a r u", a=2)
-                src = tp[:].rearrange("p a u r -> p a r u")
+                if rows_interleaved:
+                    dst = grouped[:].rearrange("p (r a) u -> p r a u", a=4)[:, :, 2 * half:2 * half + 2, :]
+                    src = tp[:].rearrange("p a u r -> p r a u")
+                else:
+                    dst = grouped[:, 2 * P * half:2 * P * (half + 1), :].rearrange("p (a r) u -> p a r u", a=2)
+                    src = tp[:].rearrange("p a u r -> p a r u")
                 if engines[half] == "s":
                     nc.scalar.copy(out=dst, in_=src)
                 else:
@@ -110,7 +115,7 @@ def tile_koslmcell_pa_t_kernel(tc, x, h_prev, c_prev, W_ih, b_ih, W_hh, b_hh,
         def t1_w(op, half):
             wv = wraw[(op, half)][:].bitcast(F32)
             srcs = [wv[:, a * (D // 2):(a + 1) * (D // 2)] for a in range(4)]
-            return transposes(srcs, "w%d%d" % (op, half), "sv")
+            return transposes(srcs, "w%d%d" % (op, half), ("ss", "vv")[op], rows_interleaved=True)
 
         def quant_w(g, op, half):
             quantise(g, wq[:, op, half * H:(half + 1) * H], wsc[:, op, half * H:(half + 1) * H])
@@ -216,15 +221,15 @@ def tile_koslmcell_pa_t_kernel(tc, x, h_prev, c_prev, W_ih, b_ih, W_hh, b_hh,
                         nc.tensor.transpose(tb[:, j * P:(j + 1) * P], tms[c][j][:, cols], ident[:])
                     nc.vector.tensor_tensor(out=ist[:, i, :], in0=tb[:], in1=mst[:, i, :], op=ALU.mult)
                     nc.scalar.mul(out=mst[:, i, :], in_=tb[:], mul=M_SCALE)
-                nc.sync.dma_start(out=outs[1][:, c * TB:(c + 1) * TB, :], in_=mst[:])
+                nc.sync.dma_start(out=dram(outs[1], c * TB, TB), in_=mst[:])
                 if b < NB:
                     final_add(c, 0, 2)
                     final_add(c, 2, 4)
-                    nc.sync.dma_start(out=outs[2][:, c * TB:(c + 1) * TB, :], in_=ist[:])
+                    nc.sync.dma_start(out=dram(outs[2], c * TB, TB), in_=ist[:])
                 else:
                     for lo in (0, 2):
                         final_add(c, lo, lo + 2)
-                        nc.sync.dma_start(out=outs[2][:, c * TB + lo:c * TB + lo + 2, :], in_=ist[:, lo:lo + 2, :])
+                        nc.sync.dma_start(out=dram(outs[2], c * TB + lo, 2), in_=ist[:, lo:lo + 2, :])
             for g in fresh:
                 quant_in(g)
             if b < NB:
@@ -243,4 +248,4 @@ def tile_koslmcell_pa_t_kernel(tc, x, h_prev, c_prev, W_ih, b_ih, W_hh, b_hh,
                                             start=(op == 0), stop=(op == 1))
                     nc.vector.tensor_tensor(out=zst[:, i, :], in0=az[:], in1=bias_z[:], op=ALU.add)
                     nc.scalar.activation(out=zst[:, i, :], in_=zst[:, i, :], func=ACT.Tanh)
-                nc.sync.dma_start(out=outs[0][:, b * TB:(b + 1) * TB, :], in_=zst[:])
+                nc.sync.dma_start(out=dram(outs[0], b * TB, TB), in_=zst[:])

@@ -32,7 +32,6 @@ def tile_koslmcell_pa_t_kernel(tc, x, h_prev, c_prev, W_ih, b_ih, W_hh, b_hh,
         tpool = ctx.enter_context(tc.tile_pool(name="tpool", bufs=8))
         stage = ctx.enter_context(tc.tile_pool(name="stage", bufs=3))
         ps = ctx.enter_context(tc.psum_pool(name="ps", bufs=8))
-        ctx.enter_context(tc.manual_schedule())
 
         def row(v):
             return v.rearrange("(o n) -> o n", o=1)

@@ -13,11 +13,15 @@ ALU = mybir.AluOpType
 
 P = 128
 B, D, H = 4096, 512, 512
-NT = B // P
-TG = 8
+WORDS = D // 2
 TB = 4
-NB = NT // TB
+TG = 8
+NB = B // (P * TB)
 M_SCALE = 1.5
+ONES_COLS = 32
+GPSIMD_SUMS = 3
+X, HP, CP = 0, 1, 2
+Z_HALF, M_HALF = 0, 1
 FLOPS = 2 * B * (2 * H) * (D + H)
 
 
@@ -32,76 +36,80 @@ def tile_koslmcell_pa_t_kernel(tc, x, h_prev, c_prev, W_ih, b_ih, W_hh, b_hh,
         tpool = ctx.enter_context(tc.tile_pool(name="tpool", bufs=8))
         stage = ctx.enter_context(tc.tile_pool(name="stage", bufs=3))
         ps = ctx.enter_context(tc.psum_pool(name="ps", bufs=8))
+        ctx.enter_context(tc.manual_schedule())
 
-        def row(v):
-            return v.rearrange("(o n) -> o n", o=1)
+        def as_row(vector):
+            return vector.rearrange("(o n) -> o n", o=1)
 
         vecs = const.tile([P, 3 * H], BF16, name="vecs")
         nc.vector.memset(vecs[:], 0.0)
         ones = const.tile([P, P], BF16, name="ones")
         nc.vector.memset(ones[:], 1.0)
-        nc.scalar.dma_start(out=vecs[0:1, 0:2 * H], in_=row(b_ih))
-        nc.scalar.dma_start(out=vecs[1:2, 0:2 * H], in_=row(b_hh))
-        nc.scalar.dma_start(out=vecs[2:3, 0:H], in_=row(z_bias))
-        nc.scalar.dma_start(out=vecs[2:3, H:2 * H], in_=row(m_bias))
-        nc.scalar.dma_start(out=vecs[0:1, 2 * H:3 * H], in_=row(log_lambda))
+        nc.scalar.dma_start(out=vecs[0:1, 0:2 * H], in_=as_row(b_ih))
+        nc.scalar.dma_start(out=vecs[1:2, 0:2 * H], in_=as_row(b_hh))
+        nc.scalar.dma_start(out=vecs[2:3, 0:H], in_=as_row(z_bias))
+        nc.scalar.dma_start(out=vecs[2:3, H:2 * H], in_=as_row(m_bias))
+        nc.scalar.dma_start(out=vecs[0:1, 2 * H:3 * H], in_=as_row(log_lambda))
         ident = const.tile([P, P], F32, name="ident")
         make_identity(nc, ident[:])
 
-        views = [v.rearrange("(g p t) k -> g p t k", p=P, t=TG) for v in (x, h_prev, c_prev)]
-        outs = [o.rearrange("(g p t) n -> g p t n", p=P, t=TG) for o in (out_0, out_1, out_2)]
+        in_views = [v.rearrange("(g p t) k -> g p t k", p=P, t=TG) for v in (x, h_prev, c_prev)]
+        out_views = [o.rearrange("(g p t) n -> g p t n", p=P, t=TG) for o in (out_0, out_1, out_2)]
 
-        def dram(view, t0, n):
-            return view[t0 // TG, :, t0 % TG:t0 % TG + n, :]
+        def row_tiles(view, first, count):
+            return view[first // TG, :, first % TG:first % TG + count, :]
+
         where = [{}, {}, {}]
 
-        def load(i, t0, n, tag):
-            rt = resid.tile([P, n * D], BF16, name="in%d_%d" % (i, t0), tag="%s%d" % ("xhc"[i], tag))
-            nc.sync.dma_start(out=rt[:].rearrange("p (t k) -> p t k", k=D), in_=dram(views[i], t0, n))
-            for j in range(n):
-                where[i][t0 + j] = (rt, j)
+        def load(which, first, count, place):
+            rows = resid.tile([P, count * D], BF16, name="in%d_%d" % (which, first), tag="%s%d" % ("xhc"[which], place))
+            nc.sync.dma_start(out=rows[:].rearrange("p (t k) -> p t k", k=D),
+                              in_=row_tiles(in_views[which], first, count))
+            for j in range(count):
+                where[which][first + j] = (rows, j)
 
-        def load_w(op, half, tag):
-            w = (W_ih, W_hh)[op]
-            wr = stage.tile([P, 4 * D], BF16, name="wraw%d%d" % (op, half), tag=tag)
-            nc.sync.dma_start(out=wr[:], in_=w[half * H:(half + 1) * H, :].rearrange("(p a) k -> p (a k)", a=4))
-            return wr
+        def load_weights(op, half, tag):
+            weight = (W_ih, W_hh)[op]
+            raw = stage.tile([P, 4 * D], BF16, name="wraw%d%d" % (op, half), tag=tag)
+            nc.sync.dma_start(out=raw[:],
+                              in_=weight[half * H:(half + 1) * H, :].rearrange("(p a) k -> p (a k)", a=4))
+            return raw
 
-        load(0, 0, 4, 0)
-        load(1, 0, 4, 0)
+        load(X, 0, 4, 0)
+        load(HP, 0, 4, 0)
         wraw = {}
-        wraw[(0, 1)] = load_w(0, 1, "zst")
-        wraw[(1, 1)] = load_w(1, 1, "ist")
-        wraw[(0, 0)] = load_w(0, 0, "zst")
-        wraw[(1, 0)] = load_w(1, 0, "ist")
-        load(0, 4, 4, 4)
-        load(1, 4, 4, 4)
-        load(2, 0, 4, 0)
-        load(0, 8, 8, 8)
-        load(1, 8, 8, 8)
-        load(2, 4, 4, 4)
-        load(0, 16, 8, 16)
-        load(1, 16, 8, 16)
-        load(2, 8, 8, 8)
-        load(2, 16, 8, 16)
+        wraw[(X, Z_HALF)] = load_weights(X, Z_HALF, "zst")
+        wraw[(HP, Z_HALF)] = load_weights(HP, Z_HALF, "ist")
+        wraw[(X, M_HALF)] = load_weights(X, M_HALF, "zst")
+        wraw[(HP, M_HALF)] = load_weights(HP, M_HALF, "ist")
+        load(X, 4, 4, 4)
+        load(HP, 4, 4, 4)
+        load(CP, 0, 4, 0)
+        load(X, 8, 8, 8)
+        load(HP, 8, 8, 8)
+        load(CP, 4, 4, 4)
+        load(X, 16, 8, 16)
+        load(HP, 16, 8, 16)
+        load(CP, 8, 8, 8)
+        load(CP, 16, 8, 16)
 
         wq = const.tile([P, 2, 2 * H], U32, name="wq", align_bytes=64)
         wsc = const.tile([P, 2, 2 * H], U8, name="wsc", align_bytes=64)
 
-        def transposes(srcs, label, engines, rows_interleaved=False):
+        def transpose_512_rows(pieces, label, engines, rows_interleaved=False):
             grouped = gpool.tile([P, 4 * P, 2], F32, name="grp_" + label, tag="grp", align_bytes=64)
-            for half in range(2):
-                tp = ps.tile([P, 2, 2, P], F32, name="tp_%s_%d" % (label, half), tag="ps")
+            for bank in range(2):
+                tp = ps.tile([P, 2, 2, P], F32, name="tp_%s_%d" % (label, bank), tag="ps")
                 for a in range(2):
                     for u in range(2):
-                        nc.tensor.transpose(tp[:, a, u, :], srcs[2 * half + a][:, u * P:(u + 1) * P], ident[:])
+                        nc.tensor.transpose(tp[:, a, u, :], pieces[2 * bank + a][:, u * P:(u + 1) * P], ident[:])
                 if rows_interleaved:
-                    dst = grouped[:].rearrange("p (r a) u -> p r a u", a=4)[:, :, 2 * half:2 * half + 2, :]
+                    dst = grouped[:].rearrange("p (r a) u -> p r a u", a=4)[:, :, 2 * bank:2 * bank + 2, :]
                     src = tp[:].rearrange("p a u r -> p r a u")
                 else:
-                    dst = grouped[:, 2 * P * half:2 * P * (half + 1), :].rearrange("p (a r) u -> p a r u", a=2)
+                    dst = grouped[:, 2 * P * bank:2 * P * (bank + 1), :].rearrange("p (a r) u -> p a r u", a=2)
                     src = tp[:].rearrange("p a u r -> p a r u")
-                if engines[half] == "s":
+                if engines[bank] == "s":
                     nc.scalar.copy(out=dst, in_=src)
                 else:
                     nc.vector.tensor_copy(out=dst, in_=src)
@@ -111,140 +119,145 @@ def tile_koslmcell_pa_t_kernel(tc, x, h_prev, c_prev, W_ih, b_ih, W_hh, b_hh,
             nc.vector.quantize_mx(out=codes.bitcast(FP8X4), scales=scales,
                                   in_=grouped[:].rearrange("p c u -> p (c u)").bitcast(BF16))
 
-        def t1_w(op, half):
-            wv = wraw[(op, half)][:].bitcast(F32)
-            srcs = [wv[:, a * (D // 2):(a + 1) * (D // 2)] for a in range(4)]
-            return transposes(srcs, "w%d%d" % (op, half), ("ss", "vv")[op], rows_interleaved=True)
+        def transpose_weights(op, half):
+            words = wraw[(op, half)][:].bitcast(F32)
+            pieces = [words[:, a * WORDS:(a + 1) * WORDS] for a in range(4)]
+            return transpose_512_rows(pieces, "w%d%d" % (op, half), ("ss", "vv")[op], rows_interleaved=True)
 
-        def quant_w(g, op, half):
-            quantise(g, wq[:, op, half * H:(half + 1) * H], wsc[:, op, half * H:(half + 1) * H])
+        def quantise_weights(grouped, op, half):
+            quantise(grouped, wq[:, op, half * H:(half + 1) * H], wsc[:, op, half * H:(half + 1) * H])
 
-        def t1_in(b, op, engines):
-            srcs = []
+        def transpose_block(b, op, engines):
+            pieces = []
             for t in range(b * TB, (b + 1) * TB):
-                rt, j = where[op][t]
-                srcs.append(rt[:].bitcast(F32)[:, j * (D // 2):(j + 1) * (D // 2)])
-            return (transposes(srcs, "b%d_%d" % (b, op), engines), b, op)
+                rows, j = where[op][t]
+                pieces.append(rows[:].bitcast(F32)[:, j * WORDS:(j + 1) * WORDS])
+            return (transpose_512_rows(pieces, "b%d_%d" % (b, op), engines), b, op)
 
-        qs = {}
+        mx_in = {}
 
-        def quant_in(gbo):
-            g, b, op = gbo
-            q = qpool.tile([P, TB * P], U32, name="q%d_%d" % (b, op), tag="q%d" % op, align_bytes=64)
-            s = qpool.tile([P, TB * P], U8, name="s%d_%d" % (b, op), tag="s%d" % op, align_bytes=64)
-            quantise(g, q[:], s[:])
-            qs[(b, op)] = (q, s)
+        def quantise_block(transposed):
+            grouped, b, op = transposed
+            codes = qpool.tile([P, TB * P], U32, name="q%d_%d" % (b, op), tag="q%d" % op, align_bytes=64)
+            scales = qpool.tile([P, TB * P], U8, name="s%d_%d" % (b, op), tag="s%d" % op, align_bytes=64)
+            quantise(grouped, codes[:], scales[:])
+            mx_in[(b, op)] = (codes, scales)
 
-        tms = {}
-        msts = {}
+        tanh_m = {}
+        m_tiles = {}
+        z_tiles = {}
+        i_tiles = {}
 
-        def scaled_c(b):
-            mst = stage.tile([P, TB, H], F32, name="mst%d" % b, tag="mst")
-            msts[b] = mst
+        def scale_c_prev(b):
+            m_tile = stage.tile([P, TB, H], F32, name="mst%d" % b, tag="mst")
+            m_tiles[b] = m_tile
             for i in range(TB):
-                ct, j = where[2][b * TB + i]
-                nc.gpsimd.tensor_tensor(out=mst[:, i, :], in0=ct[:, j * H:(j + 1) * H], in1=lam15[:], op=ALU.mult)
+                rows, j = where[CP][b * TB + i]
+                nc.vector.tensor_tensor(out=m_tile[:, i, :], in0=rows[:, j * H:(j + 1) * H], in1=lam15[:], op=ALU.mult)
 
-        def mx_m(b):
-            tms[b] = []
-            for j in range(4):
-                am = ps.tile([P, TB * P], F32, name="am%d_%d" % (b, j), tag="ps")
-                for op in range(2):
-                    q, s = qs[(b, op)]
-                    nc.tensor.matmul_mx(out=am[:],
-                                        lhsT=wq[:, op, H + j * P:H + (j + 1) * P].bitcast(FP8X4),
-                                        lhsT_scale=wsc[:, op, H + j * P:H + (j + 1) * P],
-                                        rhs=q[:].bitcast(FP8X4), rhs_scale=s[:],
-                                        start=(op == 0), stop=(op == 1))
-                tm = tpool.tile([P, TB * P], F32, name="tm%d_%d" % (b, j), tag="tm")
-                nc.scalar.activation(out=tm[:], in_=am[:], func=ACT.Tanh, bias=bias_m[:, j:j + 1])
-                tms[b].append(tm)
+        def m_half(b):
+            tanh_m[b] = []
+            for j in range(H // P):
+                gates = slice(H + j * P, H + (j + 1) * P)
+                acc = ps.tile([P, TB * P], F32, name="am%d_%d" % (b, j), tag="ps")
+                for op in (X, HP):
+                    codes, scales = mx_in[(b, op)]
+                    nc.tensor.matmul_mx(out=acc[:],
+                                        lhsT=wq[:, op, gates].bitcast(FP8X4), lhsT_scale=wsc[:, op, gates],
+                                        rhs=codes[:].bitcast(FP8X4), rhs_scale=scales[:],
+                                        start=(op == X), stop=(op == HP))
+                t_tile = tpool.tile([P, TB * P], F32, name="tm%d_%d" % (b, j), tag="tm")
+                nc.scalar.activation(out=t_tile[:], in_=acc[:], func=ACT.Tanh, bias=bias_m[:, j:j + 1])
+                tanh_m[b].append(t_tile)
 
-        gx = t1_in(0, 0, "sv")
-        gh = t1_in(0, 1, "sv")
-        quant_in(gx)
-        gwm0 = t1_w(0, 1)
-        quant_in(gh)
-        gwm1 = t1_w(1, 1)
-        quant_w(gwm0, 0, 1)
+        def z_half(b):
+            z_tile = stage.tile([P, TB, H], F32, name="zst%d" % b, tag="zst")
+            z_tiles[b] = z_tile
+            for i in range(TB):
+                rows = slice(i * P, (i + 1) * P)
+                acc = ps.tile([P, H], F32, name="az%d_%d" % (b, i), tag="ps")
+                for op in (X, HP):
+                    codes, scales = mx_in[(b, op)]
+                    nc.tensor.matmul_mx(out=acc[:],
+                                        lhsT=codes[:, rows].bitcast(FP8X4), lhsT_scale=scales[:, rows],
+                                        rhs=wq[:, op, 0:H].bitcast(FP8X4), rhs_scale=wsc[:, op, 0:H],
+                                        start=(op == X), stop=(op == HP))
+                nc.vector.tensor_tensor(out=z_tile[:, i, :], in0=acc[:], in1=bias_z[:], op=ALU.add)
+                nc.scalar.activation(out=z_tile[:, i, :], in_=z_tile[:, i, :], func=ACT.Tanh)
+            nc.sync.dma_start(out=row_tiles(out_views[0], b * TB, TB), in_=z_tile[:])
+
+        def add_z(engine, b, i):
+            engine.tensor_tensor(out=i_tiles[b][:, i, :], in0=i_tiles[b][:, i, :], in1=z_tiles[b][:, i, :], op=ALU.add)
+
+        def m_back(b):
+            i_tile = stage.tile([P, TB, H], F32, name="ist%d" % b, tag="ist")
+            i_tiles[b] = i_tile
+            m_tile = m_tiles[b]
+            for i in range(TB):
+                rows = slice(i * P, (i + 1) * P)
+                back = ps.tile([P, H], F32, name="tb%d_%d" % (b, i), tag="ps")
+                for j in range(H // P):
+                    nc.tensor.transpose(back[:, j * P:(j + 1) * P], tanh_m[b][j][:, rows], ident[:])
+                nc.vector.tensor_tensor(out=i_tile[:, i, :], in0=back[:], in1=m_tile[:, i, :], op=ALU.mult)
+                nc.scalar.mul(out=m_tile[:, i, :], in_=back[:], mul=M_SCALE)
+                if i < GPSIMD_SUMS:
+                    add_z(nc.gpsimd, b, i)
+            nc.sync.dma_start(out=row_tiles(out_views[1], b * TB, TB), in_=m_tile[:])
+
+
+        x_t = transpose_block(0, X, "sv")
+        h_t = transpose_block(0, HP, "sv")
+        quantise_block(x_t)
+        w_ih_z = transpose_weights(X, Z_HALF)
+        quantise_block(h_t)
+        w_hh_z = transpose_weights(HP, Z_HALF)
+        quantise_weights(w_ih_z, X, Z_HALF)
 
         bias_z = const.tile([P, H], F32, name="bias_z")
-        bzp = ps.tile([P, H], F32, name="bzp", tag="ps")
-        nc.tensor.matmul(out=bzp[:], lhsT=ones[:], rhs=vecs[:, 0:H], start=True, stop=True)
-        nc.vector.tensor_copy(out=bias_z[:], in_=bzp[:])
-        lmp = ps.tile([P, H], F32, name="lmp", tag="ps")
-        nc.tensor.matmul(out=lmp[:], lhsT=ones[:], rhs=vecs[:, 2 * H:3 * H], start=True, stop=True)
+        bias_z_ps = ps.tile([P, H], F32, name="bzp", tag="ps")
+        nc.tensor.matmul(out=bias_z_ps[:], lhsT=ones[:], rhs=vecs[:, 0:H], start=True, stop=True)
+        nc.vector.tensor_copy(out=bias_z[:], in_=bias_z_ps[:])
+        lam_ps = ps.tile([P, H], F32, name="lmp", tag="ps")
+        nc.tensor.matmul(out=lam_ps[:], lhsT=ones[:], rhs=vecs[:, 2 * H:3 * H], start=True, stop=True)
         lam = const.tile([P, H], F32, name="lam")
-        nc.scalar.activation(out=lam[:], in_=lmp[:], func=ACT.Exp)
+        nc.scalar.activation(out=lam[:], in_=lam_ps[:], func=ACT.Exp)
         lam15 = const.tile([P, H], F32, name="lam15")
         nc.gpsimd.tensor_scalar(out=lam15[:], in0=lam[:], scalar1=M_SCALE, scalar2=0.0, op0=ALU.mult, op1=ALU.add)
-        pp = ps.tile([P, 4, 32], F32, name="pp", tag="ps")
-        for j in range(4):
-            nc.tensor.matmul(out=pp[:, j, :], lhsT=vecs[:, H + j * P:H + (j + 1) * P], rhs=ones[:, 0:32],
-                             start=True, stop=True)
-        bias_m = const.tile([P, 4], F32, name="bias_m")
-        nc.scalar.copy(out=bias_m[:], in_=pp[:, :, 0])
-        gwz0 = t1_w(0, 0)
-        quant_w(gwm1, 1, 1)
-        gwz1 = t1_w(1, 0)
-        quant_w(gwz0, 0, 0)
+        bias_m_ps = ps.tile([P, H // P, ONES_COLS], F32, name="pp", tag="ps")
+        for j in range(H // P):
+            nc.tensor.matmul(out=bias_m_ps[:, j, :], lhsT=vecs[:, H + j * P:H + (j + 1) * P],
+                             rhs=ones[:, 0:ONES_COLS], start=True, stop=True)
+        bias_m = const.tile([P, H // P], F32, name="bias_m")
+        nc.scalar.copy(out=bias_m[:], in_=bias_m_ps[:, :, 0])
 
-        zsts = {}
-        ists = {}
-
-        def final_add(b, lo, hi):
-            nc.vector.tensor_tensor(out=ists[b][:, lo:hi, :], in0=ists[b][:, lo:hi, :], in1=zsts[b][:, lo:hi, :],
-                                    op=ALU.add)
+        w_ih_m = transpose_weights(X, M_HALF)
+        quantise_weights(w_hh_z, HP, Z_HALF)
+        w_hh_m = transpose_weights(HP, M_HALF)
+        quantise_weights(w_ih_m, X, M_HALF)
 
         for b in range(NB + 1):
-            c = b - 1
-            fresh = ()
+            transposed = ()
             if b + 1 < NB:
-                how = "sv" if b == 0 else "ss"
-                fresh = (t1_in(b + 1, 0, how), t1_in(b + 1, 1, how))
+                engines = "sv" if b == 0 else "ss"
+                transposed = (transpose_block(b + 1, X, engines), transpose_block(b + 1, HP, engines))
             if b == 0:
-                quant_w(gwz1, 1, 0)
-                load(0, 24, 4, 0)
-                load(1, 24, 4, 0)
-                load(2, 24, 8, 24)
-                load(0, 28, 4, 4)
-                load(1, 28, 4, 4)
-            if c >= 0:
-                ist = stage.tile([P, TB, H], F32, name="ist%d" % c, tag="ist")
-                ists[c] = ist
-                mst = msts[c]
-                for i in range(TB):
-                    cols = slice(i * P, (i + 1) * P)
-                    tb = ps.tile([P, H], F32, name="tb%d_%d" % (c, i), tag="ps")
-                    for j in range(4):
-                        nc.tensor.transpose(tb[:, j * P:(j + 1) * P], tms[c][j][:, cols], ident[:])
-                    nc.vector.tensor_tensor(out=ist[:, i, :], in0=tb[:], in1=mst[:, i, :], op=ALU.mult)
-                    nc.scalar.mul(out=mst[:, i, :], in_=tb[:], mul=M_SCALE)
-                nc.sync.dma_start(out=dram(outs[1], c * TB, TB), in_=mst[:])
-                if b < NB:
-                    final_add(c, 0, 2)
-                    final_add(c, 2, 4)
-                    nc.sync.dma_start(out=dram(outs[2], c * TB, TB), in_=ist[:])
-                else:
-                    for lo in (0, 2):
-                        final_add(c, lo, lo + 2)
-                        nc.sync.dma_start(out=dram(outs[2], c * TB + lo, 2), in_=ist[:, lo:lo + 2, :])
-            for g in fresh:
-                quant_in(g)
+                quantise_weights(w_hh_m, HP, M_HALF)
+                load(X, 24, 4, 0)
+                load(HP, 24, 4, 0)
+                load(CP, 24, 8, 24)
+                load(X, 28, 4, 4)
+                load(HP, 28, 4, 4)
+            if b > 0:
+                m_back(b - 1)
             if b < NB:
-                scaled_c(b)
-                mx_m(b)
-                zst = stage.tile([P, TB, H], F32, name="zst%d" % b, tag="zst")
-                zsts[b] = zst
-                for i in range(TB):
-                    cols = slice(i * P, (i + 1) * P)
-                    az = ps.tile([P, H], F32, name="az%d_%d" % (b, i), tag="ps")
-                    for op in range(2):
-                        q, s = qs[(b, op)]
-                        nc.tensor.matmul_mx(out=az[:],
-                                            lhsT=q[:, cols].bitcast(FP8X4), lhsT_scale=s[:, cols],
-                                            rhs=wq[:, op, 0:H].bitcast(FP8X4), rhs_scale=wsc[:, op, 0:H],
-                                            start=(op == 0), stop=(op == 1))
-                    nc.vector.tensor_tensor(out=zst[:, i, :], in0=az[:], in1=bias_z[:], op=ALU.add)
-                    nc.scalar.activation(out=zst[:, i, :], in_=zst[:, i, :], func=ACT.Tanh)
-                nc.sync.dma_start(out=dram(outs[0], b * TB, TB), in_=zst[:])
+                z_half(b)
+            if b > 0:
+                for i in range(GPSIMD_SUMS, TB):
+                    add_z(nc.vector, b - 1, i)
+                nc.sync.dma_start(out=row_tiles(out_views[2], (b - 1) * TB, TB), in_=i_tiles[b - 1][:])
+            if b < NB:
+                scale_c_prev(b)
+            for one in transposed:
+                quantise_block(one)
+            if b < NB:
+                m_half(b)

from contextlib import ExitStack

import concourse.mybir as mybir
from concourse.masks import make_identity

F32 = mybir.dt.float32
BF16 = mybir.dt.bfloat16
U32 = mybir.dt.uint32
U8 = mybir.dt.uint8
FP8X4 = mybir.dt.float8_e4m3fn_x4
ACT = mybir.ActivationFunctionType
ALU = mybir.AluOpType

P = 128
B, D, H = 4096, 512, 512
WORDS = D // 2
TB = 4
TG = 8
NB = B // (P * TB)
M_SCALE = 1.5
ONES_COLS = 32
GPSIMD_SUMS = 3
X, HP, CP = 0, 1, 2
Z_HALF, M_HALF = 0, 1
FLOPS = 2 * B * (2 * H) * (D + H)


def tile_koslmcell_pa_t_kernel(tc, x, h_prev, c_prev, W_ih, b_ih, W_hh, b_hh,
                                          log_lambda, z_bias, m_bias, out_0, out_1, out_2):
    nc = tc.nc
    with ExitStack() as ctx:
        const = ctx.enter_context(tc.tile_pool(name="const", bufs=1))
        resid = ctx.enter_context(tc.tile_pool(name="resid", bufs=1))
        gpool = ctx.enter_context(tc.tile_pool(name="gpool", bufs=4))
        qpool = ctx.enter_context(tc.tile_pool(name="qpool", bufs=3))
        tpool = ctx.enter_context(tc.tile_pool(name="tpool", bufs=8))
        stage = ctx.enter_context(tc.tile_pool(name="stage", bufs=3))
        ps = ctx.enter_context(tc.psum_pool(name="ps", bufs=8))
        ctx.enter_context(tc.manual_schedule())

        def as_row(vector):
            return vector.rearrange("(o n) -> o n", o=1)

        vecs = const.tile([P, 3 * H], BF16, name="vecs")
        nc.vector.memset(vecs[:], 0.0)
        ones = const.tile([P, P], BF16, name="ones")
        nc.vector.memset(ones[:], 1.0)
        nc.scalar.dma_start(out=vecs[0:1, 0:2 * H], in_=as_row(b_ih))
        nc.scalar.dma_start(out=vecs[1:2, 0:2 * H], in_=as_row(b_hh))
        nc.scalar.dma_start(out=vecs[2:3, 0:H], in_=as_row(z_bias))
        nc.scalar.dma_start(out=vecs[2:3, H:2 * H], in_=as_row(m_bias))
        nc.scalar.dma_start(out=vecs[0:1, 2 * H:3 * H], in_=as_row(log_lambda))
        ident = const.tile([P, P], F32, name="ident")
        make_identity(nc, ident[:])

        in_views = [v.rearrange("(g p t) k -> g p t k", p=P, t=TG) for v in (x, h_prev, c_prev)]
        out_views = [o.rearrange("(g p t) n -> g p t n", p=P, t=TG) for o in (out_0, out_1, out_2)]

        def row_tiles(view, first, count):
            return view[first // TG, :, first % TG:first % TG + count, :]

        where = [{}, {}, {}]

        def load(which, first, count, place):
            rows = resid.tile([P, count * D], BF16, name="in%d_%d" % (which, first), tag="%s%d" % ("xhc"[which], place))
            nc.sync.dma_start(out=rows[:].rearrange("p (t k) -> p t k", k=D),
                              in_=row_tiles(in_views[which], first, count))
            for j in range(count):
                where[which][first + j] = (rows, j)

        def load_weights(op, half, tag):
            weight = (W_ih, W_hh)[op]
            raw = stage.tile([P, 4 * D], BF16, name="wraw%d%d" % (op, half), tag=tag)
            nc.sync.dma_start(out=raw[:],
                              in_=weight[half * H:(half + 1) * H, :].rearrange("(p a) k -> p (a k)", a=4))
            return raw

        load(X, 0, 4, 0)
        load(HP, 0, 4, 0)
        wraw = {}
        wraw[(X, Z_HALF)] = load_weights(X, Z_HALF, "zst")
        wraw[(HP, Z_HALF)] = load_weights(HP, Z_HALF, "ist")
        wraw[(X, M_HALF)] = load_weights(X, M_HALF, "zst")
        wraw[(HP, M_HALF)] = load_weights(HP, M_HALF, "ist")
        load(X, 4, 4, 4)
        load(HP, 4, 4, 4)
        load(CP, 0, 4, 0)
        load(X, 8, 8, 8)
        load(HP, 8, 8, 8)
        load(CP, 4, 4, 4)
        load(X, 16, 8, 16)
        load(HP, 16, 8, 16)
        load(CP, 8, 8, 8)
        load(CP, 16, 8, 16)

        wq = const.tile([P, 2, 2 * H], U32, name="wq", align_bytes=64)
        wsc = const.tile([P, 2, 2 * H], U8, name="wsc", align_bytes=64)

        def transpose_512_rows(pieces, label, engines, rows_interleaved=False):
            grouped = gpool.tile([P, 4 * P, 2], F32, name="grp_" + label, tag="grp", align_bytes=64)
            for bank in range(2):
                tp = ps.tile([P, 2, 2, P], F32, name="tp_%s_%d" % (label, bank), tag="ps")
                for a in range(2):
                    for u in range(2):
                        nc.tensor.transpose(tp[:, a, u, :], pieces[2 * bank + a][:, u * P:(u + 1) * P], ident[:])
                if rows_interleaved:
                    dst = grouped[:].rearrange("p (r a) u -> p r a u", a=4)[:, :, 2 * bank:2 * bank + 2, :]
                    src = tp[:].rearrange("p a u r -> p r a u")
                else:
                    dst = grouped[:, 2 * P * bank:2 * P * (bank + 1), :].rearrange("p (a r) u -> p a r u", a=2)
                    src = tp[:].rearrange("p a u r -> p a r u")
                if engines[bank] == "s":
                    nc.scalar.copy(out=dst, in_=src)
                else:
                    nc.vector.tensor_copy(out=dst, in_=src)
            return grouped

        def quantise(grouped, codes, scales):
            nc.vector.quantize_mx(out=codes.bitcast(FP8X4), scales=scales,
                                  in_=grouped[:].rearrange("p c u -> p (c u)").bitcast(BF16))

        def transpose_weights(op, half):
            words = wraw[(op, half)][:].bitcast(F32)
            pieces = [words[:, a * WORDS:(a + 1) * WORDS] for a in range(4)]
            return transpose_512_rows(pieces, "w%d%d" % (op, half), ("ss", "vv")[op], rows_interleaved=True)

        def quantise_weights(grouped, op, half):
            quantise(grouped, wq[:, op, half * H:(half + 1) * H], wsc[:, op, half * H:(half + 1) * H])

        def transpose_block(b, op, engines):
            pieces = []
            for t in range(b * TB, (b + 1) * TB):
                rows, j = where[op][t]
                pieces.append(rows[:].bitcast(F32)[:, j * WORDS:(j + 1) * WORDS])
            return (transpose_512_rows(pieces, "b%d_%d" % (b, op), engines), b, op)

        mx_in = {}

        def quantise_block(transposed):
            grouped, b, op = transposed
            codes = qpool.tile([P, TB * P], U32, name="q%d_%d" % (b, op), tag="q%d" % op, align_bytes=64)
            scales = qpool.tile([P, TB * P], U8, name="s%d_%d" % (b, op), tag="s%d" % op, align_bytes=64)
            quantise(grouped, codes[:], scales[:])
            mx_in[(b, op)] = (codes, scales)

        tanh_m = {}
        m_tiles = {}
        z_tiles = {}
        i_tiles = {}

        def scale_c_prev(b):
            m_tile = stage.tile([P, TB, H], F32, name="mst%d" % b, tag="mst")
            m_tiles[b] = m_tile
            for i in range(TB):
                rows, j = where[CP][b * TB + i]
                nc.vector.tensor_tensor(out=m_tile[:, i, :], in0=rows[:, j * H:(j + 1) * H], in1=lam15[:], op=ALU.mult)

        def m_half(b):
            tanh_m[b] = []
            for j in range(H // P):
                gates = slice(H + j * P, H + (j + 1) * P)
                acc = ps.tile([P, TB * P], F32, name="am%d_%d" % (b, j), tag="ps")
                for op in (X, HP):
                    codes, scales = mx_in[(b, op)]
                    nc.tensor.matmul_mx(out=acc[:],
                                        lhsT=wq[:, op, gates].bitcast(FP8X4), lhsT_scale=wsc[:, op, gates],
                                        rhs=codes[:].bitcast(FP8X4), rhs_scale=scales[:],
                                        start=(op == X), stop=(op == HP))
                t_tile = tpool.tile([P, TB * P], F32, name="tm%d_%d" % (b, j), tag="tm")
                nc.scalar.activation(out=t_tile[:], in_=acc[:], func=ACT.Tanh, bias=bias_m[:, j:j + 1])
                tanh_m[b].append(t_tile)

        def z_half(b):
            z_tile = stage.tile([P, TB, H], F32, name="zst%d" % b, tag="zst")
            z_tiles[b] = z_tile
            for i in range(TB):
                rows = slice(i * P, (i + 1) * P)
                acc = ps.tile([P, H], F32, name="az%d_%d" % (b, i), tag="ps")
                for op in (X, HP):
                    codes, scales = mx_in[(b, op)]
                    nc.tensor.matmul_mx(out=acc[:],
                                        lhsT=codes[:, rows].bitcast(FP8X4), lhsT_scale=scales[:, rows],
                                        rhs=wq[:, op, 0:H].bitcast(FP8X4), rhs_scale=wsc[:, op, 0:H],
                                        start=(op == X), stop=(op == HP))
                nc.vector.tensor_tensor(out=z_tile[:, i, :], in0=acc[:], in1=bias_z[:], op=ALU.add)
                nc.scalar.activation(out=z_tile[:, i, :], in_=z_tile[:, i, :], func=ACT.Tanh)
            nc.sync.dma_start(out=row_tiles(out_views[0], b * TB, TB), in_=z_tile[:])

        def add_z(engine, b, i):
            engine.tensor_tensor(out=i_tiles[b][:, i, :], in0=i_tiles[b][:, i, :], in1=z_tiles[b][:, i, :], op=ALU.add)

        def m_back(b):
            i_tile = stage.tile([P, TB, H], F32, name="ist%d" % b, tag="ist")
            i_tiles[b] = i_tile
            m_tile = m_tiles[b]
            for i in range(TB):
                rows = slice(i * P, (i + 1) * P)
                back = ps.tile([P, H], F32, name="tb%d_%d" % (b, i), tag="ps")
                for j in range(H // P):
                    nc.tensor.transpose(back[:, j * P:(j + 1) * P], tanh_m[b][j][:, rows], ident[:])
                nc.vector.tensor_tensor(out=i_tile[:, i, :], in0=back[:], in1=m_tile[:, i, :], op=ALU.mult)
                nc.scalar.mul(out=m_tile[:, i, :], in_=back[:], mul=M_SCALE)
                if i < GPSIMD_SUMS:
                    add_z(nc.gpsimd, b, i)
            nc.sync.dma_start(out=row_tiles(out_views[1], b * TB, TB), in_=m_tile[:])


        x_t = transpose_block(0, X, "sv")
        h_t = transpose_block(0, HP, "sv")
        quantise_block(x_t)
        w_ih_z = transpose_weights(X, Z_HALF)
        quantise_block(h_t)
        w_hh_z = transpose_weights(HP, Z_HALF)
        quantise_weights(w_ih_z, X, Z_HALF)

        bias_z = const.tile([P, H], F32, name="bias_z")
        bias_z_ps = ps.tile([P, H], F32, name="bzp", tag="ps")
        nc.tensor.matmul(out=bias_z_ps[:], lhsT=ones[:], rhs=vecs[:, 0:H], start=True, stop=True)
        nc.vector.tensor_copy(out=bias_z[:], in_=bias_z_ps[:])
        lam_ps = ps.tile([P, H], F32, name="lmp", tag="ps")
        nc.tensor.matmul(out=lam_ps[:], lhsT=ones[:], rhs=vecs[:, 2 * H:3 * H], start=True, stop=True)
        lam = const.tile([P, H], F32, name="lam")
        nc.scalar.activation(out=lam[:], in_=lam_ps[:], func=ACT.Exp)
        lam15 = const.tile([P, H], F32, name="lam15")
        nc.gpsimd.tensor_scalar(out=lam15[:], in0=lam[:], scalar1=M_SCALE, scalar2=0.0, op0=ALU.mult, op1=ALU.add)
        bias_m_ps = ps.tile([P, H // P, ONES_COLS], F32, name="pp", tag="ps")
        for j in range(H // P):
            nc.tensor.matmul(out=bias_m_ps[:, j, :], lhsT=vecs[:, H + j * P:H + (j + 1) * P],
                             rhs=ones[:, 0:ONES_COLS], start=True, stop=True)
        bias_m = const.tile([P, H // P], F32, name="bias_m")
        nc.scalar.copy(out=bias_m[:], in_=bias_m_ps[:, :, 0])

        w_ih_m = transpose_weights(X, M_HALF)
        quantise_weights(w_hh_z, HP, Z_HALF)
        w_hh_m = transpose_weights(HP, M_HALF)
        quantise_weights(w_ih_m, X, M_HALF)

        for b in range(NB + 1):
            transposed = ()
            if b + 1 < NB:
                engines = "sv" if b == 0 else "ss"
                transposed = (transpose_block(b + 1, X, engines), transpose_block(b + 1, HP, engines))
            if b == 0:
                quantise_weights(w_hh_m, HP, M_HALF)
                load(X, 24, 4, 0)
                load(HP, 24, 4, 0)
                load(CP, 24, 8, 24)
                load(X, 28, 4, 4)
                load(HP, 28, 4, 4)
            if b > 0:
                m_back(b - 1)
            if b < NB:
                z_half(b)
            if b > 0:
                for i in range(GPSIMD_SUMS, TB):
                    add_z(nc.vector, b - 1, i)
                nc.sync.dma_start(out=row_tiles(out_views[2], (b - 1) * TB, TB), in_=i_tiles[b - 1][:])
            if b < NB:
                scale_c_prev(b)
            for one in transposed:
                quantise_block(one)
            if b < NB:
                m_half(b)
